import numpy as np
import ml_dtypes


def mxq(x, axis, fmt="e4m3"):
    dtype, down = {"e4m3": (ml_dtypes.float8_e4m3fn, 7), "e5m2": (ml_dtypes.float8_e5m2, 14)}[fmt]
    v = np.moveaxis(np.asarray(x, np.float32).astype(ml_dtypes.bfloat16).astype(np.float64), axis, -1)
    blocks = v.reshape(v.shape[:-1] + (-1, 32))
    amax = np.abs(blocks).max(-1, keepdims=True)
    byte = np.maximum(np.where(amax > 0, np.frexp(amax)[1] - 1 + 127, 0) - down, 1)
    scale = np.exp2(byte - 127.0)
    codes = (blocks / scale).astype(np.float32).astype(dtype).astype(np.float64)
    return np.moveaxis((codes * scale).reshape(v.shape), -1, axis)


WIDE = False


def mx_kscale(k):
    if not WIDE:
        return np.ones(k)
    levels = np.array([10, -10, 5, -5, 0])
    a = np.random.permutation(np.resize(levels, k // 512 * 4)).reshape(k // 512, 4)
    idx = np.arange(k)
    return np.exp2(a[idx // 512, idx % 128 // 32])


BF16 = ml_dtypes.bfloat16


def bf(x):
    return np.asarray(x, np.float32).astype(BF16)


def f64(x):
    return np.asarray(x).astype(np.float64)


E2M1 = np.array([0.0, 0.5, 1.0, 1.5, 2.0, 3.0, 4.0, 6.0, -0.0, -0.5, -1.0, -1.5, -2.0, -3.0, -4.0, -6.0])


def pack_weight(w, fmt):
    k, n = w.shape
    w = f64(bf(w)).reshape(k // 32, 32, n)
    amax = np.abs(w).max(1)
    if fmt == "e4m3":
        byte = np.frexp(amax)[1] - 1 + 127 - 7
    else:
        mant, ex = np.frexp(amax / 6.0)
        byte = np.where(mant > 0.5, ex, ex - 1) + 127
    byte = np.clip(np.where(amax > 0, byte, 1), 1, 254)
    scaled = (w * np.exp2(127.0 - byte)[:, None, :]).reshape(k, n).astype(np.float32)
    by_word = np.ascontiguousarray(scaled.reshape(k // 512, 128, 4, n).transpose(0, 1, 3, 2))
    if fmt == "e4m3":
        words = by_word.astype(ml_dtypes.float8_e4m3fn).view(np.uint8)
    else:
        c = by_word.astype(ml_dtypes.float4_e2m1fn).view(np.uint8) & 0xF
        words = c[..., 0::2] | (c[..., 1::2] << 4)
    return np.ascontiguousarray(words), np.ascontiguousarray(byte.astype(np.uint8).reshape(k // 512, 16, n))


def unpack_weight(words, scales, fmt):
    g, p, n, _ = words.shape
    if fmt == "e4m3":
        vals = np.ascontiguousarray(words).view(ml_dtypes.float8_e4m3fn).astype(np.float64)
    else:
        nib = np.empty((g, p, n, 4), np.uint8)
        nib[..., 0::2] = words & 0xF
        nib[..., 1::2] = words >> 4
        vals = E2M1[nib]
    vals = vals * np.repeat(np.exp2(scales.astype(np.float64) - 127.0), 8, axis=1)[..., None]
    return vals.transpose(0, 1, 3, 2).reshape(g * 512, n)


B, D, O1, O2, O3 = 256, 16384, 1024, 512, 128
EPS = 1e-5
FMT = "e4m3"


def mish(v):
    return v * np.tanh(np.log(1.0 + np.exp(v)))


def ln(u, g, b):
    mu = u.mean(-1, keepdims=True)
    var = np.square(u - mu).mean(-1, keepdims=True)
    return (u - mu) * (1.0 / np.sqrt(var + EPS)) * g + b


def setup_inputs():
    s = mx_kscale(D)
    x = bf(np.random.uniform(0.0, 1.0, (B, D)) * s)
    w1 = np.random.standard_normal((O1, D)) * 1.5 / np.sqrt(D) / s
    W1_words, W1_scales = pack_weight(np.ascontiguousarray(w1.T), FMT)
    g1 = bf(1.0 + 0.1 * np.random.standard_normal(O1))
    b1 = bf(0.1 * np.random.standard_normal(O1))
    w2 = np.random.standard_normal((O2, O1)) * 1.5 / np.sqrt(O1)
    W2_words, W2_scales = pack_weight(np.ascontiguousarray(w2.T), FMT)
    g2 = bf(1.0 + 0.1 * np.random.standard_normal(O2))
    b2 = bf(0.1 * np.random.standard_normal(O2))
    return {"x": x,
            "W1_words": W1_words,
            "W1_scales": W1_scales,
            "g1": g1,
            "b1": b1,
            "W2_words": W2_words,
            "W2_scales": W2_scales,
            "g2": g2,
            "b2": b2}


def reference(x, W1_words, W1_scales, g1, b1, W2_words, W2_scales, g2, b2):
    u1 = mxq(f64(x), 1, "e4m3") @ unpack_weight(W1_words, W1_scales, FMT)
    h1 = mish(ln(u1, f64(g1), f64(b1)))
    u2 = mxq(h1, 1, "e4m3") @ unpack_weight(W2_words, W2_scales, FMT)
    return mish(ln(u2, f64(g2), f64(b2)))

@@ -1,0 +1,297 @@
+import concourse.mybir as mybir
+from concourse.masks import make_identity
+
+F32 = mybir.dt.float32
+BF16 = mybir.dt.bfloat16
+I32 = mybir.dt.int32
+U32 = mybir.dt.uint32
+U8 = mybir.dt.uint8
+FP8X4 = mybir.dt.float8_e4m3fn_x4
+ALU = mybir.AluOpType
+ACT = mybir.ActivationFunctionType
+
+P = 128
+PACK = 4
+K_PASS = P * PACK
+N_PASS = 512
+
+TOKENS, D_IN, D_HID, D_OUT = 256, 16384, 1024, 512
+EPS = 1e-5
+FLOPS = 2 * TOKENS * D_IN * D_HID + 2 * TOKENS * D_HID * D_OUT
+
+TOKEN_TILES = TOKENS // P
+PASSES_1 = D_IN // K_PASS
+PASSES_2 = D_HID // K_PASS
+HALVES_1 = D_HID // N_PASS
+
+X_CHUNK_K = 4096
+X_CHUNK_PASSES = X_CHUNK_K // K_PASS
+X_CHUNKS_PER_TILE = D_IN // X_CHUNK_K
+X_CHUNKS = TOKEN_TILES * X_CHUNKS_PER_TILE
+BANK_PASSES = 2
+W_CHUNK_PASSES = 2
+W_CHUNKS = PASSES_1 // W_CHUNK_PASSES
+STREAM_BUFS = 12
+PLANES_PER_TILE = 4
+QUADRANTS = 4
+EXP_CAP = 2.0**62
+
+
+def tile_autoencoder_pa_k_kernel(tc, x, W1_words, W1_scales, g1, b1, W2_words, W2_scales, g2, b2, out):
+    nc = tc.nc
+
+    def empty_bank(index, dst, src):
+        if index % 4 == 3:
+            nc.vector.tensor_copy(out=dst, in_=src)
+        else:
+            nc.scalar.copy(out=dst, in_=src)
+
+    with tc.manual_schedule(), tc.tile_pool(name="keep", bufs=1) as keep, tc.tile_pool(
+        name="stream", bufs=STREAM_BUFS
+    ) as stream, tc.psum_pool(name="turn", bufs=4) as turn, tc.psum_pool(name="sums", bufs=1) as sums:
+        ident_f32 = keep.tile([P, P], F32, name="ident_f32")
+        ident_bf16 = keep.tile([P, P], BF16, name="ident_bf16")
+        neg_half = keep.tile([P, 1], F32, name="neg_half")
+        table_warm = keep.tile([P, 1], F32, name="table_warm")
+        nc.gpsimd.memset(neg_half[:], -0.5)
+        make_identity(nc, ident_f32[:])
+        make_identity(nc, ident_bf16[:])
+
+        x_codes = keep.tile([P, TOKEN_TILES, PASSES_1 * P], U32, name="x_codes", align_bytes=64)
+        x_scales = keep.tile([P, TOKEN_TILES, PASSES_1 * P], U8, name="x_scales", align_bytes=64)
+        w1_planes = keep.tile([P, PASSES_1 // PLANES_PER_TILE, D_HID], U8, name="w1_planes", align_bytes=64)
+        w2_words = keep.tile([P, PASSES_2, D_OUT], U32, name="w2_words", align_bytes=64)
+        w2_planes = keep.tile([P, D_OUT], U8, name="w2_planes", align_bytes=64)
+        h_codes = keep.tile([P, TOKEN_TILES, PASSES_2 * P], U32, name="h_codes", align_bytes=64)
+        h_scales = keep.tile([P, TOKEN_TILES, PASSES_2 * P], U8, name="h_scales", align_bytes=64)
+        g1_all = keep.tile([P, HALVES_1, N_PASS], F32, name="g1_all")
+        b1_all = keep.tile([P, HALVES_1, N_PASS], F32, name="b1_all")
+        g2_all = keep.tile([P, D_OUT], F32, name="g2_all")
+        b2_all = keep.tile([P, D_OUT], F32, name="b2_all")
+
+        def load_w1_chunk(j):
+            chunk = stream.tile([P, W_CHUNK_PASSES, D_HID], U32, name="w1_chunk", tag="stream", align_bytes=64)
+            passes = W1_words[j * W_CHUNK_PASSES : (j + 1) * W_CHUNK_PASSES]
+            nc.sync.dma_start(
+                out=chunk[:].bitcast(I32), in_=passes.rearrange("g p n t -> p g (n t)").bitcast(I32)
+            )
+            return chunk
+
+        with tc.tile_pool(name="stage", bufs=3) as stage:
+            x_chunks = []
+            for c in range(X_CHUNKS):
+                m, part = divmod(c, X_CHUNKS_PER_TILE)
+                x_chunk = stream.tile([P, X_CHUNK_K], BF16, name="x_chunk", tag="stream", align_bytes=64)
+                nc.sync.dma_start(
+                    out=x_chunk[:], in_=x[m * P : (m + 1) * P, part * X_CHUNK_K : (part + 1) * X_CHUNK_K]
+                )
+                x_chunks.append(x_chunk)
+
+            rows = stage.tile([P, 2 * D_HID + 2 * D_OUT], BF16, name="rows", bufs=1)
+            ones = stage.tile([P, P], BF16, name="ones", bufs=1)
+            nc.vector.memset(rows[:].bitcast(I32), 0)
+            nc.vector.memset(ones[:], 1.0)
+            first = 0
+            for vector in (g1, b1, g2, b2):
+                width = vector.shape[0]
+                nc.scalar.dma_start(out=rows[0:1, first : first + width], in_=vector.unsqueeze(0))
+                first += width
+            nc.scalar.activation(out=table_warm[:], in_=neg_half[:], func=ACT.Exp)
+
+            nc.vector.memset(w1_planes[:].bitcast(I32), 0)
+            nc.vector.memset(w2_planes[:].bitcast(I32), 0)
+            for s in range(PASSES_1 // PLANES_PER_TILE):
+                for quadrant in range(QUADRANTS):
+                    nc.sync.dma_start(
+                        out=w1_planes[32 * quadrant : 32 * quadrant + 16, s, :].bitcast(I32),
+                        in_=W1_scales[
+                            PLANES_PER_TILE * s : PLANES_PER_TILE * (s + 1), 4 * quadrant : 4 * quadrant + 4, :
+                        ].bitcast(I32),
+                    )
+            nc.sync.dma_start(
+                out=w2_words[:].bitcast(I32), in_=W2_words.rearrange("g p n t -> p g (n t)").bitcast(I32)
+            )
+            for quadrant in range(QUADRANTS):
+                nc.sync.dma_start(
+                    out=w2_planes[32 * quadrant : 32 * quadrant + 4 * PASSES_2, :].bitcast(I32),
+                    in_=W2_scales[:, 4 * quadrant : 4 * quadrant + 4, :].bitcast(I32),
+                )
+            w1_chunks = [load_w1_chunk(j) for j in range(STREAM_BUFS - X_CHUNKS)]
+
+            def quantise_x_chunk(c, grouped):
+                m, part = divmod(c, X_CHUNKS_PER_TILE)
+                columns = slice(part * X_CHUNK_PASSES * P, (part + 1) * X_CHUNK_PASSES * P)
+                nc.vector.quantize_mx(
+                    out=x_codes[:, m, columns].bitcast(FP8X4), scales=x_scales[:, m, columns], in_=grouped[:]
+                )
+
+            waiting = None
+            for c in range(X_CHUNKS):
+                words = x_chunks[c][:].bitcast(F32)
+                grouped = stage.tile([P, X_CHUNK_K], BF16, name="grouped", align_bytes=64)
+                grouped_words = grouped[:].bitcast(F32).rearrange("p (g r u) -> p g r u", g=X_CHUNK_PASSES, u=2)
+                for bank in range(X_CHUNK_PASSES // BANK_PASSES):
+                    turned = turn.tile([P, BANK_PASSES, 2, P], F32, name="turned", tag="turn")
+                    for i in range(BANK_PASSES):
+                        first_word = (bank * BANK_PASSES + i) * (K_PASS // 2)
+                        for u in range(2):
+                            nc.tensor.transpose(
+                                turned[:, i, u, :], words[:, first_word + u : first_word + K_PASS // 2 : 2], ident_f32[:]
+                            )
+                    empty_bank(
+                        bank,
+                        grouped_words[:, bank * BANK_PASSES : (bank + 1) * BANK_PASSES, :, :],
+                        turned[:].rearrange("p g u r -> p g r u"),
+                    )
+                w1_chunks.append(load_w1_chunk(len(w1_chunks)))
+                if waiting is not None:
+                    quantise_x_chunk(*waiting)
+                waiting = (c, grouped)
+            quantise_x_chunk(*waiting)
+
+            spread = (
+                (g1_all[:, 0, :], True),
+                (g1_all[:, 1, :], True),
+                (b1_all[:, 0, :], True),
+                (b1_all[:, 1, :], True),
+                (g2_all[:], False),
+                (b2_all[:], False),
+            )
+            for i, (target, by_word_byte) in enumerate(spread):
+                repeated = turn.tile([P, N_PASS], F32, name="repeated", tag="turn")
+                nc.tensor.matmul(
+                    out=repeated[:], lhsT=ones[:], rhs=rows[:, i * N_PASS : (i + 1) * N_PASS], start=True, stop=True
+                )
+                if by_word_byte:
+                    nc.vector.tensor_copy(
+                        out=target.rearrange("p (t q) -> p t q", t=PACK),
+                        in_=repeated[:].rearrange("p (q t) -> p t q", t=PACK),
+                    )
+                else:
+                    nc.vector.tensor_copy(out=target, in_=repeated[:])
+
+        u1 = [
+            [sums.tile([P, N_PASS], F32, name="u1_%d%d" % (m, h), tag="sum%d%d" % (m, h)) for h in range(HALVES_1)]
+            for m in range(TOKEN_TILES)
+        ]
+        for j in range(W_CHUNKS):
+            for m in range(TOKEN_TILES):
+                for i in range(W_CHUNK_PASSES):
+                    g = j * W_CHUNK_PASSES + i
+                    offset = 4 * (g % PLANES_PER_TILE)
+                    for h in range(HALVES_1):
+                        features = slice(h * N_PASS, (h + 1) * N_PASS)
+                        nc.tensor.matmul_mx(
+                            out=u1[m][h][:],
+                            lhsT=x_codes[:, m, g * P : (g + 1) * P].bitcast(FP8X4),
+                            lhsT_scale=x_scales[:, m, g * P : (g + 1) * P],
+                            rhs=w1_chunks[j][:, i, features].bitcast(FP8X4),
+                            rhs_scale=w1_planes[offset:P, g // PLANES_PER_TILE, features],
+                            start=(g == 0),
+                            stop=(g == PASSES_1 - 1),
+                        )
+            if len(w1_chunks) < W_CHUNKS:
+                w1_chunks.append(load_w1_chunk(len(w1_chunks)))
+
+        with tc.tile_pool(name="tail", bufs=1) as tail:
+
+            def row_statistics(label, banks):
+                partial = tail.tile([P, len(banks), 6], F32, name="partial_" + label)
+                for i, bank in enumerate(banks):
+                    nc.vector.bn_stats(out=partial[:, i, :], in_=bank[:])
+                mean_var = tail.tile([P, 2], F32, name="mean_var_" + label)
+                nc.vector.bn_aggr(out=mean_var[:], in_=partial[:].rearrange("p b s -> p (b s)"))
+                var_eps = tail.tile([P, 1], F32, name="var_eps_" + label)
+                nc.vector.tensor_scalar_add(out=var_eps[:], in0=mean_var[:, 1:2], scalar1=EPS)
+                rstd = tail.tile([P, 1], F32, name="rstd_" + label)
+                nc.gpsimd.tensor_tensor(out=rstd[:], in0=var_eps[:], in1=neg_half[:], op=ALU.pow)
+                return mean_var[:, 0:1], rstd[:]
+
+            pieces = [(m, g) for m in range(TOKEN_TILES) for g in range(PASSES_2)]
+            stats_1 = [row_statistics("1%d" % m, u1[m]) for m in range(TOKEN_TILES)]
+            v1 = [tail.tile([P, PASSES_2, N_PASS], F32, name="v1_%d" % m) for m in range(TOKEN_TILES)]
+            gate1 = [tail.tile([P, PASSES_2, N_PASS], F32, name="gate1_%d" % m) for m in range(TOKEN_TILES)]
+            h1 = [tail.tile([P, PASSES_2, PACK, P], BF16, name="h1_%d" % m) for m in range(TOKEN_TILES)]
+            for m, g in pieces:
+                mean, rstd = stats_1[m]
+                centred = tail.tile([P, PACK, P], F32, name="centred", bufs=2)
+                nc.vector.scalar_tensor_tensor(
+                    out=centred[:],
+                    in0=u1[m][g][:].rearrange("p (q t) -> p t q", t=PACK),
+                    scalar=mean,
+                    in1=g1_all[:, g, :].rearrange("p (t q) -> p t q", t=PACK),
+                    op0=ALU.subtract,
+                    op1=ALU.mult,
+                )
+                nc.vector.scalar_tensor_tensor(
+                    out=v1[m][:, g, :],
+                    in0=centred[:].rearrange("p t q -> p (t q)"),
+                    scalar=rstd,
+                    in1=b1_all[:, g, :],
+                    op0=ALU.mult,
+                    op1=ALU.add,
+                )
+                nc.scalar.activation(out=gate1[m][:, g, :], in_=v1[m][:, g, :], func=ACT.Exp)
+            for m, g in pieces:
+                nc.vector.tensor_scalar(
+                    out=gate1[m][:, g, :], in0=gate1[m][:, g, :], scalar1=EXP_CAP, scalar2=1.0, op0=ALU.min, op1=ALU.add
+                )
+            for m, g in pieces:
+                nc.scalar.activation(out=gate1[m][:, g, :], in_=gate1[m][:, g, :], func=ACT.Ln)
+            turned_h = []
+            for m, g in pieces:
+                nc.scalar.activation(out=gate1[m][:, g, :], in_=gate1[m][:, g, :], func=ACT.Tanh)
+                nc.vector.tensor_mul(
+                    out=h1[m][:, g, :, :].rearrange("p t q -> p (t q)"), in0=v1[m][:, g, :], in1=gate1[m][:, g, :]
+                )
+                turned = turn.tile([P, PACK, P], BF16, name="turned_h", tag="turn")
+                for t in range(PACK):
+                    nc.tensor.transpose(turned[:, t, :], h1[m][:, g, t, :], ident_bf16[:])
+                turned_h.append(turned)
+
+            grouped_h = [tail.tile([P, PASSES_2, P, PACK], BF16, name="grouped_h%d" % m, align_bytes=64) for m in range(TOKEN_TILES)]
+            for i, (m, g) in enumerate(pieces):
+                empty_bank(i, grouped_h[m][:, g, :, :], turned_h[i][:].rearrange("p t r -> p r t"))
+            u2 = []
+            for m in range(TOKEN_TILES):
+                nc.vector.quantize_mx(
+                    out=h_codes[:, m, :].bitcast(FP8X4),
+                    scales=h_scales[:, m, :],
+                    in_=grouped_h[m][:].rearrange("p g r t -> p (g r t)"),
+                )
+                u2_m = sums.tile([P, D_OUT], F32, name="u2_%d" % m, tag="sum%d0" % m)
+                for g in range(PASSES_2):
+                    nc.tensor.matmul_mx(
+                        out=u2_m[:],
+                        lhsT=h_codes[:, m, g * P : (g + 1) * P].bitcast(FP8X4),
+                        lhsT_scale=h_scales[:, m, g * P : (g + 1) * P],
+                        rhs=w2_words[:, g, :].bitcast(FP8X4),
+                        rhs_scale=w2_planes[4 * g : P, :],
+                        start=(g == 0),
+                        stop=(g == PASSES_2 - 1),
+                    )
+                u2.append(u2_m)
+
+            stats_2 = [row_statistics("2%d" % m, [u2[m]]) for m in range(TOKEN_TILES)]
+            v2 = [tail.tile([P, D_OUT], F32, name="v2_%d" % m) for m in range(TOKEN_TILES)]
+            gate2 = [tail.tile([P, D_OUT], F32, name="gate2_%d" % m) for m in range(TOKEN_TILES)]
+            for m in range(TOKEN_TILES):
+                mean, rstd = stats_2[m]
+                centred = tail.tile([P, D_OUT], F32, name="centred", bufs=2)
+                nc.vector.scalar_tensor_tensor(
+                    out=centred[:], in0=u2[m][:], scalar=mean, in1=g2_all[:], op0=ALU.subtract, op1=ALU.mult
+                )
+                nc.vector.scalar_tensor_tensor(
+                    out=v2[m][:], in0=centred[:], scalar=rstd, in1=b2_all[:], op0=ALU.mult, op1=ALU.add
+                )
+                nc.scalar.activation(out=gate2[m][:], in_=v2[m][:], func=ACT.Exp)
+            for m in range(TOKEN_TILES):
+                nc.vector.tensor_scalar(
+                    out=gate2[m][:], in0=gate2[m][:], scalar1=EXP_CAP, scalar2=1.0, op0=ALU.min, op1=ALU.add
+                )
+            for m in range(TOKEN_TILES):
+                nc.scalar.activation(out=gate2[m][:], in_=gate2[m][:], func=ACT.Ln)
+            for m in range(TOKEN_TILES):
+                nc.scalar.activation(out=gate2[m][:], in_=gate2[m][:], func=ACT.Tanh)
+                nc.vector.tensor_mul(out=v2[m][:], in0=v2[m][:], in1=gate2[m][:])
+                nc.sync.dma_start(out=out[m * P : (m + 1) * P, :], in_=v2[m][:])

@@ -31,7 +31,7 @@ X_CHUNKS = TOKEN_TILES * X_CHUNKS_PER_TILE
 BANK_PASSES = 2
 W_CHUNK_PASSES = 2
 W_CHUNKS = PASSES_1 // W_CHUNK_PASSES
-STREAM_BUFS = 12
+STREAM_BUFS = 14
 PLANES_PER_TILE = 4
 QUADRANTS = 4
 EXP_CAP = 2.0**62
@@ -55,7 +55,6 @@ def tile_autoencoder_pa_k_kernel(tc, x, W1_words, W1_scales, g1, b1, W2_words, W
         table_warm = keep.tile([P, 1], F32, name="table_warm")
         nc.gpsimd.memset(neg_half[:], -0.5)
         make_identity(nc, ident_f32[:])
-        make_identity(nc, ident_bf16[:])
 
         x_codes = keep.tile([P, TOKEN_TILES, PASSES_1 * P], U32, name="x_codes", align_bytes=64)
         x_scales = keep.tile([P, TOKEN_TILES, PASSES_1 * P], U8, name="x_scales", align_bytes=64)
@@ -69,12 +68,28 @@ def tile_autoencoder_pa_k_kernel(tc, x, W1_words, W1_scales, g1, b1, W2_words, W
         g2_all = keep.tile([P, D_OUT], F32, name="g2_all")
         b2_all = keep.tile([P, D_OUT], F32, name="b2_all")
 
+        nc.vector.memset(w1_planes[:].bitcast(I32), 0)
+        nc.vector.memset(w2_planes[:].bitcast(I32), 0)
+        for quadrant in range(QUADRANTS):
+            for r in range(4):
+                nc.gpsimd.dma_start(
+                    out=w1_planes[32 * quadrant + r : 32 * quadrant + 16 : 4, :, :].bitcast(F32),
+                    in_=W1_scales[:, 4 * quadrant + r, :].rearrange("(s j) n -> j s n", j=PLANES_PER_TILE).bitcast(F32),
+                )
+        for quadrant in range(QUADRANTS):
+            nc.gpsimd.dma_start(
+                out=w2_planes[32 * quadrant : 32 * quadrant + 4 * PASSES_2, :].bitcast(F32),
+                in_=W2_scales[:, 4 * quadrant : 4 * quadrant + 4, :].bitcast(F32),
+            )
+        make_identity(nc, ident_bf16[:])
+
         def load_w1_chunk(j):
             chunk = stream.tile([P, W_CHUNK_PASSES, D_HID], U32, name="w1_chunk", tag="stream", align_bytes=64)
-            passes = W1_words[j * W_CHUNK_PASSES : (j + 1) * W_CHUNK_PASSES]
-            nc.sync.dma_start(
-                out=chunk[:].bitcast(I32), in_=passes.rearrange("g p n t -> p g (n t)").bitcast(I32)
-            )
+            for i in range(W_CHUNK_PASSES):
+                nc.sync.dma_start(
+                    out=chunk[:, i, :].bitcast(I32),
+                    in_=W1_words[j * W_CHUNK_PASSES + i].rearrange("p n t -> p (n t)").bitcast(I32),
+                )
             return chunk
 
         with tc.tile_pool(name="stage", bufs=3) as stage:
@@ -98,24 +113,9 @@ def tile_autoencoder_pa_k_kernel(tc, x, W1_words, W1_scales, g1, b1, W2_words, W
                 first += width
             nc.scalar.activation(out=table_warm[:], in_=neg_half[:], func=ACT.Exp)
 
-            nc.vector.memset(w1_planes[:].bitcast(I32), 0)
-            nc.vector.memset(w2_planes[:].bitcast(I32), 0)
-            for s in range(PASSES_1 // PLANES_PER_TILE):
-                for quadrant in range(QUADRANTS):
-                    nc.sync.dma_start(
-                        out=w1_planes[32 * quadrant : 32 * quadrant + 16, s, :].bitcast(I32),
-                        in_=W1_scales[
-                            PLANES_PER_TILE * s : PLANES_PER_TILE * (s + 1), 4 * quadrant : 4 * quadrant + 4, :
-                        ].bitcast(I32),
-                    )
             nc.sync.dma_start(
                 out=w2_words[:].bitcast(I32), in_=W2_words.rearrange("g p n t -> p g (n t)").bitcast(I32)
             )
-            for quadrant in range(QUADRANTS):
-                nc.sync.dma_start(
-                    out=w2_planes[32 * quadrant : 32 * quadrant + 4 * PASSES_2, :].bitcast(I32),
-                    in_=W2_scales[:, 4 * quadrant : 4 * quadrant + 4, :].bitcast(I32),
-                )
             w1_chunks = [load_w1_chunk(j) for j in range(STREAM_BUFS - X_CHUNKS)]
 
             def quantise_x_chunk(c, grouped):
@@ -175,10 +175,10 @@ def tile_autoencoder_pa_k_kernel(tc, x, W1_words, W1_scales, g1, b1, W2_words, W
             for m in range(TOKEN_TILES)
         ]
         for j in range(W_CHUNKS):
-            for m in range(TOKEN_TILES):
-                for i in range(W_CHUNK_PASSES):
-                    g = j * W_CHUNK_PASSES + i
-                    offset = 4 * (g % PLANES_PER_TILE)
+            for i in range(W_CHUNK_PASSES):
+                g = j * W_CHUNK_PASSES + i
+                offset = 4 * (g % PLANES_PER_TILE)
+                for m in range(TOKEN_TILES):
                     for h in range(HALVES_1):
                         features = slice(h * N_PASS, (h + 1) * N_PASS)
                         nc.tensor.matmul_mx(

@@ -31,10 +31,10 @@ X_CHUNKS = TOKEN_TILES * X_CHUNKS_PER_TILE
 BANK_PASSES = 2
 W_CHUNK_PASSES = 2
 W_CHUNKS = PASSES_1 // W_CHUNK_PASSES
-STREAM_BUFS = 14
+STREAM_BUFS = 12
 PLANES_PER_TILE = 4
 QUADRANTS = 4
-EXP_CAP = 2.0**62
+SQRT_2 = 2.0**0.5
 
 
 def tile_autoencoder_pa_k_kernel(tc, x, W1_words, W1_scales, g1, b1, W2_words, W2_scales, g2, b2, out):
@@ -51,10 +51,13 @@ def tile_autoencoder_pa_k_kernel(tc, x, W1_words, W1_scales, g1, b1, W2_words, W
     ) as stream, tc.psum_pool(name="turn", bufs=4) as turn, tc.psum_pool(name="sums", bufs=1) as sums:
         ident_f32 = keep.tile([P, P], F32, name="ident_f32")
         ident_bf16 = keep.tile([P, P], BF16, name="ident_bf16")
-        neg_half = keep.tile([P, 1], F32, name="neg_half")
+        eps_col = keep.tile([P, 1], F32, name="eps_col")
+        two_col = keep.tile([P, 1], F32, name="two_col")
         table_warm = keep.tile([P, 1], F32, name="table_warm")
-        nc.gpsimd.memset(neg_half[:], -0.5)
+        nc.gpsimd.memset(eps_col[:], EPS)
+        nc.gpsimd.memset(two_col[:], 2.0)
         make_identity(nc, ident_f32[:])
+        make_identity(nc, ident_bf16[:])
 
         x_codes = keep.tile([P, TOKEN_TILES, PASSES_1 * P], U32, name="x_codes", align_bytes=64)
         x_scales = keep.tile([P, TOKEN_TILES, PASSES_1 * P], U8, name="x_scales", align_bytes=64)
@@ -63,33 +66,17 @@ def tile_autoencoder_pa_k_kernel(tc, x, W1_words, W1_scales, g1, b1, W2_words, W
         w2_planes = keep.tile([P, D_OUT], U8, name="w2_planes", align_bytes=64)
         h_codes = keep.tile([P, TOKEN_TILES, PASSES_2 * P], U32, name="h_codes", align_bytes=64)
         h_scales = keep.tile([P, TOKEN_TILES, PASSES_2 * P], U8, name="h_scales", align_bytes=64)
-        g1_all = keep.tile([P, HALVES_1, N_PASS], F32, name="g1_all")
+        minus_g1_all = keep.tile([P, HALVES_1, N_PASS], F32, name="minus_g1_all")
         b1_all = keep.tile([P, HALVES_1, N_PASS], F32, name="b1_all")
-        g2_all = keep.tile([P, D_OUT], F32, name="g2_all")
+        minus_g2_all = keep.tile([P, D_OUT], F32, name="minus_g2_all")
         b2_all = keep.tile([P, D_OUT], F32, name="b2_all")
-
-        nc.vector.memset(w1_planes[:].bitcast(I32), 0)
-        nc.vector.memset(w2_planes[:].bitcast(I32), 0)
-        for quadrant in range(QUADRANTS):
-            for r in range(4):
-                nc.gpsimd.dma_start(
-                    out=w1_planes[32 * quadrant + r : 32 * quadrant + 16 : 4, :, :].bitcast(F32),
-                    in_=W1_scales[:, 4 * quadrant + r, :].rearrange("(s j) n -> j s n", j=PLANES_PER_TILE).bitcast(F32),
-                )
-        for quadrant in range(QUADRANTS):
-            nc.gpsimd.dma_start(
-                out=w2_planes[32 * quadrant : 32 * quadrant + 4 * PASSES_2, :].bitcast(F32),
-                in_=W2_scales[:, 4 * quadrant : 4 * quadrant + 4, :].bitcast(F32),
-            )
-        make_identity(nc, ident_bf16[:])
 
         def load_w1_chunk(j):
             chunk = stream.tile([P, W_CHUNK_PASSES, D_HID], U32, name="w1_chunk", tag="stream", align_bytes=64)
-            for i in range(W_CHUNK_PASSES):
-                nc.sync.dma_start(
-                    out=chunk[:, i, :].bitcast(I32),
-                    in_=W1_words[j * W_CHUNK_PASSES + i].rearrange("p n t -> p (n t)").bitcast(I32),
-                )
+            passes = W1_words[j * W_CHUNK_PASSES : (j + 1) * W_CHUNK_PASSES]
+            nc.sync.dma_start(
+                out=chunk[:].bitcast(I32), in_=passes.rearrange("g p n t -> p g (n t)").bitcast(I32)
+            )
             return chunk
 
         with tc.tile_pool(name="stage", bufs=3) as stage:
@@ -111,11 +98,26 @@ def tile_autoencoder_pa_k_kernel(tc, x, W1_words, W1_scales, g1, b1, W2_words, W
                 width = vector.shape[0]
                 nc.scalar.dma_start(out=rows[0:1, first : first + width], in_=vector.unsqueeze(0))
                 first += width
-            nc.scalar.activation(out=table_warm[:], in_=neg_half[:], func=ACT.Exp)
+            nc.scalar.activation(out=table_warm[:], in_=two_col[:], func=ACT.Abs_reciprocal_sqrt)
 
+            nc.vector.memset(w1_planes[:].bitcast(I32), 0)
+            nc.vector.memset(w2_planes[:].bitcast(I32), 0)
+            for s in range(PASSES_1 // PLANES_PER_TILE):
+                for quadrant in range(QUADRANTS):
+                    nc.sync.dma_start(
+                        out=w1_planes[32 * quadrant : 32 * quadrant + 16, s, :].bitcast(I32),
+                        in_=W1_scales[
+                            PLANES_PER_TILE * s : PLANES_PER_TILE * (s + 1), 4 * quadrant : 4 * quadrant + 4, :
+                        ].bitcast(I32),
+                    )
             nc.sync.dma_start(
                 out=w2_words[:].bitcast(I32), in_=W2_words.rearrange("g p n t -> p g (n t)").bitcast(I32)
             )
+            for quadrant in range(QUADRANTS):
+                nc.sync.dma_start(
+                    out=w2_planes[32 * quadrant : 32 * quadrant + 4 * PASSES_2, :].bitcast(I32),
+                    in_=W2_scales[:, 4 * quadrant : 4 * quadrant + 4, :].bitcast(I32),
+                )
             w1_chunks = [load_w1_chunk(j) for j in range(STREAM_BUFS - X_CHUNKS)]
 
             def quantise_x_chunk(c, grouped):
@@ -150,35 +152,33 @@ def tile_autoencoder_pa_k_kernel(tc, x, W1_words, W1_scales, g1, b1, W2_words, W
             quantise_x_chunk(*waiting)
 
             spread = (
-                (g1_all[:, 0, :], True),
-                (g1_all[:, 1, :], True),
-                (b1_all[:, 0, :], True),
-                (b1_all[:, 1, :], True),
-                (g2_all[:], False),
-                (b2_all[:], False),
+                (minus_g1_all[:, 0, :], -1.0, "p (q t) -> p t q"),
+                (minus_g1_all[:, 1, :], -1.0, "p (q t) -> p t q"),
+                (b1_all[:, 0, :], 1.0, "p (q t) -> p t q"),
+                (b1_all[:, 1, :], 1.0, "p (q t) -> p t q"),
+                (minus_g2_all[:], -1.0, "p (t q) -> p t q"),
+                (b2_all[:], 1.0, "p (t q) -> p t q"),
             )
-            for i, (target, by_word_byte) in enumerate(spread):
+            for i, (target, sign, order) in enumerate(spread):
                 repeated = turn.tile([P, N_PASS], F32, name="repeated", tag="turn")
                 nc.tensor.matmul(
                     out=repeated[:], lhsT=ones[:], rhs=rows[:, i * N_PASS : (i + 1) * N_PASS], start=True, stop=True
                 )
-                if by_word_byte:
-                    nc.vector.tensor_copy(
-                        out=target.rearrange("p (t q) -> p t q", t=PACK),
-                        in_=repeated[:].rearrange("p (q t) -> p t q", t=PACK),
-                    )
-                else:
-                    nc.vector.tensor_copy(out=target, in_=repeated[:])
+                nc.vector.tensor_scalar_mul(
+                    out=target.rearrange("p (t q) -> p t q", t=PACK),
+                    in0=repeated[:].rearrange(order, t=PACK),
+                    scalar1=sign,
+                )
 
         u1 = [
             [sums.tile([P, N_PASS], F32, name="u1_%d%d" % (m, h), tag="sum%d%d" % (m, h)) for h in range(HALVES_1)]
             for m in range(TOKEN_TILES)
         ]
         for j in range(W_CHUNKS):
-            for i in range(W_CHUNK_PASSES):
-                g = j * W_CHUNK_PASSES + i
-                offset = 4 * (g % PLANES_PER_TILE)
-                for m in range(TOKEN_TILES):
+            for m in range(TOKEN_TILES):
+                for i in range(W_CHUNK_PASSES):
+                    g = j * W_CHUNK_PASSES + i
+                    offset = 4 * (g % PLANES_PER_TILE)
                     for h in range(HALVES_1):
                         features = slice(h * N_PASS, (h + 1) * N_PASS)
                         nc.tensor.matmul_mx(
@@ -201,57 +201,79 @@ def tile_autoencoder_pa_k_kernel(tc, x, W1_words, W1_scales, g1, b1, W2_words, W
                     nc.vector.bn_stats(out=partial[:, i, :], in_=bank[:])
                 mean_var = tail.tile([P, 2], F32, name="mean_var_" + label)
                 nc.vector.bn_aggr(out=mean_var[:], in_=partial[:].rearrange("p b s -> p (b s)"))
-                var_eps = tail.tile([P, 1], F32, name="var_eps_" + label)
-                nc.vector.tensor_scalar_add(out=var_eps[:], in0=mean_var[:, 1:2], scalar1=EPS)
                 rstd = tail.tile([P, 1], F32, name="rstd_" + label)
-                nc.gpsimd.tensor_tensor(out=rstd[:], in0=var_eps[:], in1=neg_half[:], op=ALU.pow)
+                nc.scalar.activation(out=rstd[:], in_=mean_var[:, 1:2], func=ACT.Abs_reciprocal_sqrt, bias=eps_col[:])
                 return mean_var[:, 0:1], rstd[:]
 
-            pieces = [(m, g) for m in range(TOKEN_TILES) for g in range(PASSES_2)]
+            def norm_and_mish(pieces, after):
+                work = []
+                for u, (mean, rstd), minus_gain, bias, result, m in pieces:
+                    centred = tail.tile([P, PACK, P], F32, name="centred", bufs=2)
+                    minus_v = tail.tile([P, N_PASS], F32, name="minus_v", bufs=4)
+                    gate = tail.tile([P, N_PASS], F32, name="gate", bufs=4)
+                    nc.vector.scalar_tensor_tensor(
+                        out=centred[:], in0=u, scalar=mean, in1=minus_gain, op0=ALU.subtract, op1=ALU.mult
+                    )
+                    nc.vector.scalar_tensor_tensor(
+                        out=minus_v[:],
+                        in0=centred[:].rearrange("p t q -> p (t q)"),
+                        scalar=rstd,
+                        in1=bias,
+                        op0=ALU.mult,
+                        op1=ALU.subtract,
+                    )
+                    nc.scalar.activation(out=gate[:], in_=minus_v[:], func=ACT.Exp, scale=-1.0)
+                    work.append((minus_v, gate, result, m))
+                for minus_v, gate, result, m in work:
+                    nc.vector.scalar_tensor_tensor(
+                        out=gate[:], in0=gate[:], scalar=2.0, in1=gate[:], op0=ALU.add, op1=ALU.mult
+                    )
+                for minus_v, gate, result, m in work:
+                    nc.scalar.activation(out=gate[:], in_=gate[:], func=ACT.Abs_reciprocal_sqrt, bias=two_col[:])
+                for i, (minus_v, gate, result, m) in enumerate(work):
+                    if m == 0:
+                        nc.vector.scalar_tensor_tensor(
+                            out=gate[:], in0=gate[:], scalar=2.0, in1=gate[:], op0=ALU.mult, op1=ALU.mult
+                        )
+                    else:
+                        nc.scalar.activation(out=gate[:], in_=gate[:], func=ACT.Square, scale=SQRT_2)
+                    nc.vector.scalar_tensor_tensor(
+                        out=result, in0=gate[:], scalar=1.0, in1=minus_v[:], op0=ALU.subtract, op1=ALU.mult
+                    )
+                    after(i)
+
             stats_1 = [row_statistics("1%d" % m, u1[m]) for m in range(TOKEN_TILES)]
-            v1 = [tail.tile([P, PASSES_2, N_PASS], F32, name="v1_%d" % m) for m in range(TOKEN_TILES)]
-            gate1 = [tail.tile([P, PASSES_2, N_PASS], F32, name="gate1_%d" % m) for m in range(TOKEN_TILES)]
             h1 = [tail.tile([P, PASSES_2, PACK, P], BF16, name="h1_%d" % m) for m in range(TOKEN_TILES)]
-            for m, g in pieces:
-                mean, rstd = stats_1[m]
-                centred = tail.tile([P, PACK, P], F32, name="centred", bufs=2)
-                nc.vector.scalar_tensor_tensor(
-                    out=centred[:],
-                    in0=u1[m][g][:].rearrange("p (q t) -> p t q", t=PACK),
-                    scalar=mean,
-                    in1=g1_all[:, g, :].rearrange("p (t q) -> p t q", t=PACK),
-                    op0=ALU.subtract,
-                    op1=ALU.mult,
+            pieces_1 = [
+                (
+                    u1[m][g][:].rearrange("p (q t) -> p t q", t=PACK),
+                    stats_1[m],
+                    minus_g1_all[:, g, :].rearrange("p (t q) -> p t q", t=PACK),
+                    b1_all[:, g, :],
+                    h1[m][:, g, :, :].rearrange("p t q -> p (t q)"),
+                    m,
                 )
-                nc.vector.scalar_tensor_tensor(
-                    out=v1[m][:, g, :],
-                    in0=centred[:].rearrange("p t q -> p (t q)"),
-                    scalar=rstd,
-                    in1=b1_all[:, g, :],
-                    op0=ALU.mult,
-                    op1=ALU.add,
-                )
-                nc.scalar.activation(out=gate1[m][:, g, :], in_=v1[m][:, g, :], func=ACT.Exp)
-            for m, g in pieces:
-                nc.vector.tensor_scalar(
-                    out=gate1[m][:, g, :], in0=gate1[m][:, g, :], scalar1=EXP_CAP, scalar2=1.0, op0=ALU.min, op1=ALU.add
-                )
-            for m, g in pieces:
-                nc.scalar.activation(out=gate1[m][:, g, :], in_=gate1[m][:, g, :], func=ACT.Ln)
+                for m in range(TOKEN_TILES)
+                for g in range(PASSES_2)
+            ]
             turned_h = []
-            for m, g in pieces:
-                nc.scalar.activation(out=gate1[m][:, g, :], in_=gate1[m][:, g, :], func=ACT.Tanh)
-                nc.vector.tensor_mul(
-                    out=h1[m][:, g, :, :].rearrange("p t q -> p (t q)"), in0=v1[m][:, g, :], in1=gate1[m][:, g, :]
-                )
+
+            def transpose_h1(i):
+                m, g = divmod(i, PASSES_2)
                 turned = turn.tile([P, PACK, P], BF16, name="turned_h", tag="turn")
                 for t in range(PACK):
                     nc.tensor.transpose(turned[:, t, :], h1[m][:, g, t, :], ident_bf16[:])
                 turned_h.append(turned)
 
-            grouped_h = [tail.tile([P, PASSES_2, P, PACK], BF16, name="grouped_h%d" % m, align_bytes=64) for m in range(TOKEN_TILES)]
-            for i, (m, g) in enumerate(pieces):
-                empty_bank(i, grouped_h[m][:, g, :, :], turned_h[i][:].rearrange("p t r -> p r t"))
+            norm_and_mish(pieces_1, transpose_h1)
+
+            grouped_h = [
+                tail.tile([P, PASSES_2, P, PACK], BF16, name="grouped_h%d" % m, align_bytes=64)
+                for m in range(TOKEN_TILES)
+            ]
+            for i, turned in enumerate(turned_h):
+                m, g = divmod(i, PASSES_2)
+                empty_bank(i, grouped_h[m][:, g, :, :], turned[:].rearrange("p t r -> p r t"))
             u2 = []
             for m in range(TOKEN_TILES):
                 nc.vector.quantize_mx(
@@ -273,25 +295,20 @@ def tile_autoencoder_pa_k_kernel(tc, x, W1_words, W1_scales, g1, b1, W2_words, W
                 u2.append(u2_m)
 
             stats_2 = [row_statistics("2%d" % m, [u2[m]]) for m in range(TOKEN_TILES)]
-            v2 = [tail.tile([P, D_OUT], F32, name="v2_%d" % m) for m in range(TOKEN_TILES)]
-            gate2 = [tail.tile([P, D_OUT], F32, name="gate2_%d" % m) for m in range(TOKEN_TILES)]
-            for m in range(TOKEN_TILES):
-                mean, rstd = stats_2[m]
-                centred = tail.tile([P, D_OUT], F32, name="centred", bufs=2)
-                nc.vector.scalar_tensor_tensor(
-                    out=centred[:], in0=u2[m][:], scalar=mean, in1=g2_all[:], op0=ALU.subtract, op1=ALU.mult
+            mish_2 = [tail.tile([P, D_OUT], F32, name="mish_2_%d" % m) for m in range(TOKEN_TILES)]
+            pieces_2 = [
+                (
+                    u2[m][:].rearrange("p (t q) -> p t q", t=PACK),
+                    stats_2[m],
+                    minus_g2_all[:].rearrange("p (t q) -> p t q", t=PACK),
+                    b2_all[:],
+                    mish_2[m][:],
+                    m,
                 )
-                nc.vector.scalar_tensor_tensor(
-                    out=v2[m][:], in0=centred[:], scalar=rstd, in1=b2_all[:], op0=ALU.mult, op1=ALU.add
-                )
-                nc.scalar.activation(out=gate2[m][:], in_=v2[m][:], func=ACT.Exp)
-            for m in range(TOKEN_TILES):
-                nc.vector.tensor_scalar(
-                    out=gate2[m][:], in0=gate2[m][:], scalar1=EXP_CAP, scalar2=1.0, op0=ALU.min, op1=ALU.add
-                )
-            for m in range(TOKEN_TILES):
-                nc.scalar.activation(out=gate2[m][:], in_=gate2[m][:], func=ACT.Ln)
-            for m in range(TOKEN_TILES):
-                nc.scalar.activation(out=gate2[m][:], in_=gate2[m][:], func=ACT.Tanh)
-                nc.vector.tensor_mul(out=v2[m][:], in0=v2[m][:], in1=gate2[m][:])
-                nc.sync.dma_start(out=out[m * P : (m + 1) * P, :], in_=v2[m][:])
+                for m in range(TOKEN_TILES)
+            ]
+
+            def store_result(m):
+                nc.sync.dma_start(out=out[m * P : (m + 1) * P, :], in_=mish_2[m][:])
+
+            norm_and_mish(pieces_2, store_result)

@@ -31,7 +31,7 @@ X_CHUNKS = TOKEN_TILES * X_CHUNKS_PER_TILE
 BANK_PASSES = 2
 W_CHUNK_PASSES = 2
 W_CHUNKS = PASSES_1 // W_CHUNK_PASSES
-STREAM_BUFS = 12
+STREAM_BUFS = 14
 PLANES_PER_TILE = 4
 QUADRANTS = 4
 SQRT_2 = 2.0**0.5
@@ -73,22 +73,14 @@ def tile_autoencoder_pa_k_kernel(tc, x, W1_words, W1_scales, g1, b1, W2_words, W
 
         def load_w1_chunk(j):
             chunk = stream.tile([P, W_CHUNK_PASSES, D_HID], U32, name="w1_chunk", tag="stream", align_bytes=64)
-            passes = W1_words[j * W_CHUNK_PASSES : (j + 1) * W_CHUNK_PASSES]
-            nc.sync.dma_start(
-                out=chunk[:].bitcast(I32), in_=passes.rearrange("g p n t -> p g (n t)").bitcast(I32)
-            )
+            for i in range(W_CHUNK_PASSES):
+                nc.sync.dma_start(
+                    out=chunk[:, i, :].bitcast(I32),
+                    in_=W1_words[j * W_CHUNK_PASSES + i].rearrange("p n t -> p (n t)").bitcast(I32),
+                )
             return chunk
 
         with tc.tile_pool(name="stage", bufs=3) as stage:
-            x_chunks = []
-            for c in range(X_CHUNKS):
-                m, part = divmod(c, X_CHUNKS_PER_TILE)
-                x_chunk = stream.tile([P, X_CHUNK_K], BF16, name="x_chunk", tag="stream", align_bytes=64)
-                nc.sync.dma_start(
-                    out=x_chunk[:], in_=x[m * P : (m + 1) * P, part * X_CHUNK_K : (part + 1) * X_CHUNK_K]
-                )
-                x_chunks.append(x_chunk)
-
             rows = stage.tile([P, 2 * D_HID + 2 * D_OUT], BF16, name="rows", bufs=1)
             ones = stage.tile([P, P], BF16, name="ones", bufs=1)
             nc.vector.memset(rows[:].bitcast(I32), 0)
@@ -100,24 +92,25 @@ def tile_autoencoder_pa_k_kernel(tc, x, W1_words, W1_scales, g1, b1, W2_words, W
                 first += width
             nc.scalar.activation(out=table_warm[:], in_=two_col[:], func=ACT.Abs_reciprocal_sqrt)
 
+            x_chunks = []
+            for c in range(X_CHUNKS):
+                m, part = divmod(c, X_CHUNKS_PER_TILE)
+                x_chunk = stream.tile([P, X_CHUNK_K], BF16, name="x_chunk", tag="stream", align_bytes=64)
+                nc.sync.dma_start(
+                    out=x_chunk[:], in_=x[m * P : (m + 1) * P, part * X_CHUNK_K : (part + 1) * X_CHUNK_K]
+                )
+                x_chunks.append(x_chunk)
+
             nc.vector.memset(w1_planes[:].bitcast(I32), 0)
             nc.vector.memset(w2_planes[:].bitcast(I32), 0)
-            for s in range(PASSES_1 // PLANES_PER_TILE):
-                for quadrant in range(QUADRANTS):
-                    nc.sync.dma_start(
-                        out=w1_planes[32 * quadrant : 32 * quadrant + 16, s, :].bitcast(I32),
-                        in_=W1_scales[
-                            PLANES_PER_TILE * s : PLANES_PER_TILE * (s + 1), 4 * quadrant : 4 * quadrant + 4, :
-                        ].bitcast(I32),
-                    )
-            nc.sync.dma_start(
-                out=w2_words[:].bitcast(I32), in_=W2_words.rearrange("g p n t -> p g (n t)").bitcast(I32)
-            )
             for quadrant in range(QUADRANTS):
-                nc.sync.dma_start(
-                    out=w2_planes[32 * quadrant : 32 * quadrant + 4 * PASSES_2, :].bitcast(I32),
-                    in_=W2_scales[:, 4 * quadrant : 4 * quadrant + 4, :].bitcast(I32),
-                )
+                for r in range(4):
+                    nc.sync.dma_start(
+                        out=w1_planes[32 * quadrant + r : 32 * quadrant + 16 : 4, :, :].bitcast(I32),
+                        in_=W1_scales[:, 4 * quadrant + r, :]
+                        .rearrange("(s j) n -> j s n", j=PLANES_PER_TILE)
+                        .bitcast(I32),
+                    )
             w1_chunks = [load_w1_chunk(j) for j in range(STREAM_BUFS - X_CHUNKS)]
 
             def quantise_x_chunk(c, grouped):
@@ -175,10 +168,10 @@ def tile_autoencoder_pa_k_kernel(tc, x, W1_words, W1_scales, g1, b1, W2_words, W
             for m in range(TOKEN_TILES)
         ]
         for j in range(W_CHUNKS):
-            for m in range(TOKEN_TILES):
-                for i in range(W_CHUNK_PASSES):
-                    g = j * W_CHUNK_PASSES + i
-                    offset = 4 * (g % PLANES_PER_TILE)
+            for i in range(W_CHUNK_PASSES):
+                g = j * W_CHUNK_PASSES + i
+                offset = 4 * (g % PLANES_PER_TILE)
+                for m in range(TOKEN_TILES):
                     for h in range(HALVES_1):
                         features = slice(h * N_PASS, (h + 1) * N_PASS)
                         nc.tensor.matmul_mx(
@@ -192,6 +185,12 @@ def tile_autoencoder_pa_k_kernel(tc, x, W1_words, W1_scales, g1, b1, W2_words, W
                         )
             if len(w1_chunks) < W_CHUNKS:
                 w1_chunks.append(load_w1_chunk(len(w1_chunks)))
+        nc.sync.dma_start(out=w2_words[:].bitcast(I32), in_=W2_words.rearrange("g p n t -> p g (n t)").bitcast(I32))
+        for quadrant in range(QUADRANTS):
+            nc.sync.dma_start(
+                out=w2_planes[32 * quadrant : 32 * quadrant + 4 * PASSES_2, :].bitcast(I32),
+                in_=W2_scales[:, 4 * quadrant : 4 * quadrant + 4, :].bitcast(I32),
+            )
 
         with tc.tile_pool(name="tail", bufs=1) as tail:
 

@@ -41,7 +41,7 @@ def tile_autoencoder_pa_k_kernel(tc, x, W1_words, W1_scales, g1, b1, W2_words, W
     nc = tc.nc
 
     def empty_bank(index, dst, src):
-        if index % 4 == 3:
+        if index % 4 == 2:
             nc.vector.tensor_copy(out=dst, in_=src)
         else:
             nc.scalar.copy(out=dst, in_=src)
@@ -57,7 +57,6 @@ def tile_autoencoder_pa_k_kernel(tc, x, W1_words, W1_scales, g1, b1, W2_words, W
         nc.gpsimd.memset(eps_col[:], EPS)
         nc.gpsimd.memset(two_col[:], 2.0)
         make_identity(nc, ident_f32[:])
-        make_identity(nc, ident_bf16[:])
 
         x_codes = keep.tile([P, TOKEN_TILES, PASSES_1 * P], U32, name="x_codes", align_bytes=64)
         x_scales = keep.tile([P, TOKEN_TILES, PASSES_1 * P], U8, name="x_scales", align_bytes=64)
@@ -71,6 +70,23 @@ def tile_autoencoder_pa_k_kernel(tc, x, W1_words, W1_scales, g1, b1, W2_words, W
         minus_g2_all = keep.tile([P, D_OUT], F32, name="minus_g2_all")
         b2_all = keep.tile([P, D_OUT], F32, name="b2_all")
 
+        nc.vector.memset(w1_planes[:].bitcast(I32), 0)
+        nc.vector.memset(w2_planes[:].bitcast(I32), 0)
+        for s in range(PASSES_1 // PLANES_PER_TILE):
+            for quadrant in range(QUADRANTS):
+                nc.gpsimd.dma_start(
+                    out=w1_planes[32 * quadrant : 32 * quadrant + 16, s, :].bitcast(F32),
+                    in_=W1_scales[
+                        PLANES_PER_TILE * s : PLANES_PER_TILE * (s + 1), 4 * quadrant : 4 * quadrant + 4, :
+                    ].bitcast(F32),
+                )
+        for quadrant in range(QUADRANTS):
+            nc.gpsimd.dma_start(
+                out=w2_planes[32 * quadrant : 32 * quadrant + 4 * PASSES_2, :].bitcast(F32),
+                in_=W2_scales[:, 4 * quadrant : 4 * quadrant + 4, :].bitcast(F32),
+            )
+        make_identity(nc, ident_bf16[:])
+
         def load_w1_chunk(j):
             chunk = stream.tile([P, W_CHUNK_PASSES, D_HID], U32, name="w1_chunk", tag="stream", align_bytes=64)
             for i in range(W_CHUNK_PASSES):
@@ -81,8 +97,8 @@ def tile_autoencoder_pa_k_kernel(tc, x, W1_words, W1_scales, g1, b1, W2_words, W
             return chunk
 
         with tc.tile_pool(name="stage", bufs=3) as stage:
-            rows = stage.tile([P, 2 * D_HID + 2 * D_OUT], BF16, name="rows", bufs=1)
-            ones = stage.tile([P, P], BF16, name="ones", bufs=1)
+            rows = keep.tile([P, 2 * D_HID + 2 * D_OUT], BF16, name="rows")
+            ones = keep.tile([P, P], BF16, name="ones")
             nc.vector.memset(rows[:].bitcast(I32), 0)
             nc.vector.memset(ones[:], 1.0)
             first = 0
@@ -101,17 +117,19 @@ def tile_autoencoder_pa_k_kernel(tc, x, W1_words, W1_scales, g1, b1, W2_words, W
                 )
                 x_chunks.append(x_chunk)
 
-            nc.vector.memset(w1_planes[:].bitcast(I32), 0)
-            nc.vector.memset(w2_planes[:].bitcast(I32), 0)
-            for quadrant in range(QUADRANTS):
-                for r in range(4):
-                    nc.sync.dma_start(
-                        out=w1_planes[32 * quadrant + r : 32 * quadrant + 16 : 4, :, :].bitcast(I32),
-                        in_=W1_scales[:, 4 * quadrant + r, :]
-                        .rearrange("(s j) n -> j s n", j=PLANES_PER_TILE)
-                        .bitcast(I32),
-                    )
             w1_chunks = [load_w1_chunk(j) for j in range(STREAM_BUFS - X_CHUNKS)]
+
+            def repeat_on_all_partitions(block, target, sign, order, on_scalar):
+                repeated = turn.tile([P, N_PASS], F32, name="repeated", tag="turn")
+                nc.tensor.matmul(
+                    out=repeated[:], lhsT=ones[:], rhs=rows[:, block * N_PASS : (block + 1) * N_PASS], start=True, stop=True
+                )
+                dst = target.rearrange("p (t q) -> p t q", t=PACK)
+                src = repeated[:].rearrange(order, t=PACK)
+                if on_scalar:
+                    nc.scalar.mul(out=dst, in_=src, mul=sign)
+                else:
+                    nc.vector.tensor_scalar_mul(out=dst, in0=src, scalar1=sign)
 
             def quantise_x_chunk(c, grouped):
                 m, part = divmod(c, X_CHUNKS_PER_TILE)
@@ -138,30 +156,15 @@ def tile_autoencoder_pa_k_kernel(tc, x, W1_words, W1_scales, g1, b1, W2_words, W
                         grouped_words[:, bank * BANK_PASSES : (bank + 1) * BANK_PASSES, :, :],
                         turned[:].rearrange("p g u r -> p g r u"),
                     )
+                if c == 0:
+                    for h in range(HALVES_1):
+                        repeat_on_all_partitions(h, minus_g1_all[:, h, :], -1.0, "p (q t) -> p t q", False)
+                        repeat_on_all_partitions(HALVES_1 + h, b1_all[:, h, :], 1.0, "p (q t) -> p t q", False)
                 w1_chunks.append(load_w1_chunk(len(w1_chunks)))
                 if waiting is not None:
                     quantise_x_chunk(*waiting)
                 waiting = (c, grouped)
             quantise_x_chunk(*waiting)
-
-            spread = (
-                (minus_g1_all[:, 0, :], -1.0, "p (q t) -> p t q"),
-                (minus_g1_all[:, 1, :], -1.0, "p (q t) -> p t q"),
-                (b1_all[:, 0, :], 1.0, "p (q t) -> p t q"),
-                (b1_all[:, 1, :], 1.0, "p (q t) -> p t q"),
-                (minus_g2_all[:], -1.0, "p (t q) -> p t q"),
-                (b2_all[:], 1.0, "p (t q) -> p t q"),
-            )
-            for i, (target, sign, order) in enumerate(spread):
-                repeated = turn.tile([P, N_PASS], F32, name="repeated", tag="turn")
-                nc.tensor.matmul(
-                    out=repeated[:], lhsT=ones[:], rhs=rows[:, i * N_PASS : (i + 1) * N_PASS], start=True, stop=True
-                )
-                nc.vector.tensor_scalar_mul(
-                    out=target.rearrange("p (t q) -> p t q", t=PACK),
-                    in0=repeated[:].rearrange(order, t=PACK),
-                    scalar1=sign,
-                )
 
         u1 = [
             [sums.tile([P, N_PASS], F32, name="u1_%d%d" % (m, h), tag="sum%d%d" % (m, h)) for h in range(HALVES_1)]
@@ -186,11 +189,6 @@ def tile_autoencoder_pa_k_kernel(tc, x, W1_words, W1_scales, g1, b1, W2_words, W
             if len(w1_chunks) < W_CHUNKS:
                 w1_chunks.append(load_w1_chunk(len(w1_chunks)))
         nc.sync.dma_start(out=w2_words[:].bitcast(I32), in_=W2_words.rearrange("g p n t -> p g (n t)").bitcast(I32))
-        for quadrant in range(QUADRANTS):
-            nc.sync.dma_start(
-                out=w2_planes[32 * quadrant : 32 * quadrant + 4 * PASSES_2, :].bitcast(I32),
-                in_=W2_scales[:, 4 * quadrant : 4 * quadrant + 4, :].bitcast(I32),
-            )
 
         with tc.tile_pool(name="tail", bufs=1) as tail:
 
@@ -242,6 +240,8 @@ def tile_autoencoder_pa_k_kernel(tc, x, W1_words, W1_scales, g1, b1, W2_words, W
                     after(i)
 
             stats_1 = [row_statistics("1%d" % m, u1[m]) for m in range(TOKEN_TILES)]
+            repeat_on_all_partitions(2 * HALVES_1, minus_g2_all[:], -1.0, "p (t q) -> p t q", True)
+            repeat_on_all_partitions(2 * HALVES_1 + 1, b2_all[:], 1.0, "p (t q) -> p t q", True)
             h1 = [tail.tile([P, PASSES_2, PACK, P], BF16, name="h1_%d" % m) for m in range(TOKEN_TILES)]
             pieces_1 = [
                 (

@@ -34,6 +34,7 @@ W_CHUNKS = PASSES_1 // W_CHUNK_PASSES
 STREAM_BUFS = 14
 PLANES_PER_TILE = 4
 QUADRANTS = 4
+PAIR = 2
 SQRT_2 = 2.0**0.5
 
 
@@ -192,54 +193,68 @@ def tile_autoencoder_pa_k_kernel(tc, x, W1_words, W1_scales, g1, b1, W2_words, W
 
         with tc.tile_pool(name="tail", bufs=1) as tail:
 
-            def row_statistics(label, banks):
-                partial = tail.tile([P, len(banks), 6], F32, name="partial_" + label)
-                for i, bank in enumerate(banks):
-                    nc.vector.bn_stats(out=partial[:, i, :], in_=bank[:])
-                mean_var = tail.tile([P, 2], F32, name="mean_var_" + label)
-                nc.vector.bn_aggr(out=mean_var[:], in_=partial[:].rearrange("p b s -> p (b s)"))
-                rstd = tail.tile([P, 1], F32, name="rstd_" + label)
-                nc.scalar.activation(out=rstd[:], in_=mean_var[:, 1:2], func=ACT.Abs_reciprocal_sqrt, bias=eps_col[:])
-                return mean_var[:, 0:1], rstd[:]
+            def row_statistics(label, rows_of_banks):
+                partials = []
+                for m, banks in enumerate(rows_of_banks):
+                    partial = tail.tile([P, len(banks), 6], F32, name="partial_%s%d" % (label, m))
+                    for i, bank in enumerate(banks):
+                        nc.vector.bn_stats(out=partial[:, i, :], in_=bank[:])
+                    partials.append(partial)
+                statistics = []
+                for m, partial in enumerate(partials):
+                    mean_var = tail.tile([P, 2], F32, name="mean_var_%s%d" % (label, m))
+                    nc.vector.bn_aggr(out=mean_var[:], in_=partial[:].rearrange("p b s -> p (b s)"))
+                    rstd = tail.tile([P, 1], F32, name="rstd_%s%d" % (label, m))
+                    nc.scalar.activation(
+                        out=rstd[:], in_=mean_var[:, 1:2], func=ACT.Abs_reciprocal_sqrt, bias=eps_col[:]
+                    )
+                    statistics.append((mean_var[:, 0:1], rstd[:]))
+                return statistics
 
             def norm_and_mish(pieces, after):
                 work = []
-                for u, (mean, rstd), minus_gain, bias, result, m in pieces:
-                    centred = tail.tile([P, PACK, P], F32, name="centred", bufs=2)
-                    minus_v = tail.tile([P, N_PASS], F32, name="minus_v", bufs=4)
-                    gate = tail.tile([P, N_PASS], F32, name="gate", bufs=4)
-                    nc.vector.scalar_tensor_tensor(
-                        out=centred[:], in0=u, scalar=mean, in1=minus_gain, op0=ALU.subtract, op1=ALU.mult
-                    )
-                    nc.vector.scalar_tensor_tensor(
-                        out=minus_v[:],
-                        in0=centred[:].rearrange("p t q -> p (t q)"),
-                        scalar=rstd,
-                        in1=bias,
-                        op0=ALU.mult,
-                        op1=ALU.subtract,
-                    )
-                    nc.scalar.activation(out=gate[:], in_=minus_v[:], func=ACT.Exp, scale=-1.0)
-                    work.append((minus_v, gate, result, m))
+                for first in range(0, len(pieces), PAIR):
+                    pair = pieces[first : first + PAIR]
+                    centred_pair = []
+                    for u, (mean, rstd), minus_gain, bias, result, m in pair:
+                        centred = tail.tile([P, PACK, P], F32, name="centred", bufs=PAIR)
+                        nc.vector.scalar_tensor_tensor(
+                            out=centred[:], in0=u, scalar=mean, in1=minus_gain, op0=ALU.subtract, op1=ALU.mult
+                        )
+                        centred_pair.append(centred)
+                    for centred, (u, (mean, rstd), minus_gain, bias, result, m) in zip(centred_pair, pair):
+                        minus_v = tail.tile([P, N_PASS], F32, name="minus_v", bufs=4)
+                        gate = tail.tile([P, N_PASS], F32, name="gate", bufs=4)
+                        nc.vector.scalar_tensor_tensor(
+                            out=minus_v[:],
+                            in0=centred[:].rearrange("p t q -> p (t q)"),
+                            scalar=rstd,
+                            in1=bias,
+                            op0=ALU.mult,
+                            op1=ALU.subtract,
+                        )
+                        nc.scalar.activation(out=gate[:], in_=minus_v[:], func=ACT.Exp, scale=-1.0)
+                        work.append((minus_v, gate, result, m))
                 for minus_v, gate, result, m in work:
                     nc.vector.scalar_tensor_tensor(
                         out=gate[:], in0=gate[:], scalar=2.0, in1=gate[:], op0=ALU.add, op1=ALU.mult
                     )
                 for minus_v, gate, result, m in work:
                     nc.scalar.activation(out=gate[:], in_=gate[:], func=ACT.Abs_reciprocal_sqrt, bias=two_col[:])
-                for i, (minus_v, gate, result, m) in enumerate(work):
+                for minus_v, gate, result, m in work:
                     if m == 0:
                         nc.vector.scalar_tensor_tensor(
                             out=gate[:], in0=gate[:], scalar=2.0, in1=gate[:], op0=ALU.mult, op1=ALU.mult
                         )
                     else:
                         nc.scalar.activation(out=gate[:], in_=gate[:], func=ACT.Square, scale=SQRT_2)
+                for i, (minus_v, gate, result, m) in enumerate(work):
                     nc.vector.scalar_tensor_tensor(
                         out=result, in0=gate[:], scalar=1.0, in1=minus_v[:], op0=ALU.subtract, op1=ALU.mult
                     )
                     after(i)
 
-            stats_1 = [row_statistics("1%d" % m, u1[m]) for m in range(TOKEN_TILES)]
+            stats_1 = row_statistics("1", u1)
             repeat_on_all_partitions(2 * HALVES_1, minus_g2_all[:], -1.0, "p (t q) -> p t q", True)
             repeat_on_all_partitions(2 * HALVES_1 + 1, b2_all[:], 1.0, "p (t q) -> p t q", True)
             h1 = [tail.tile([P, PASSES_2, PACK, P], BF16, name="h1_%d" % m) for m in range(TOKEN_TILES)]
@@ -293,7 +308,7 @@ def tile_autoencoder_pa_k_kernel(tc, x, W1_words, W1_scales, g1, b1, W2_words, W
                     )
                 u2.append(u2_m)
 
-            stats_2 = [row_statistics("2%d" % m, [u2[m]]) for m in range(TOKEN_TILES)]
+            stats_2 = row_statistics("2", [[u2_m] for u2_m in u2])
             mish_2 = [tail.tile([P, D_OUT], F32, name="mish_2_%d" % m) for m in range(TOKEN_TILES)]
             pieces_2 = [
                 (

@@ -34,7 +34,7 @@ W_CHUNKS = PASSES_1 // W_CHUNK_PASSES
 STREAM_BUFS = 14
 PLANES_PER_TILE = 4
 QUADRANTS = 4
-PAIR = 2
+TILE_BY_TILE_CHUNKS = 3
 SQRT_2 = 2.0**0.5
 
 
@@ -52,10 +52,10 @@ def tile_autoencoder_pa_k_kernel(tc, x, W1_words, W1_scales, g1, b1, W2_words, W
     ) as stream, tc.psum_pool(name="turn", bufs=4) as turn, tc.psum_pool(name="sums", bufs=1) as sums:
         ident_f32 = keep.tile([P, P], F32, name="ident_f32")
         ident_bf16 = keep.tile([P, P], BF16, name="ident_bf16")
-        eps_col = keep.tile([P, 1], F32, name="eps_col")
+        minus_half = keep.tile([P, 1], F32, name="minus_half")
         two_col = keep.tile([P, 1], F32, name="two_col")
         table_warm = keep.tile([P, 1], F32, name="table_warm")
-        nc.gpsimd.memset(eps_col[:], EPS)
+        nc.gpsimd.memset(minus_half[:], -0.5)
         nc.gpsimd.memset(two_col[:], 2.0)
         make_identity(nc, ident_f32[:])
 
@@ -107,7 +107,7 @@ def tile_autoencoder_pa_k_kernel(tc, x, W1_words, W1_scales, g1, b1, W2_words, W
                 width = vector.shape[0]
                 nc.scalar.dma_start(out=rows[0:1, first : first + width], in_=vector.unsqueeze(0))
                 first += width
-            nc.scalar.activation(out=table_warm[:], in_=two_col[:], func=ACT.Abs_reciprocal_sqrt)
+            nc.scalar.activation(out=table_warm[:], in_=two_col[:], func=ACT.Exp)
 
             x_chunks = []
             for c in range(X_CHUNKS):
@@ -161,6 +161,8 @@ def tile_autoencoder_pa_k_kernel(tc, x, W1_words, W1_scales, g1, b1, W2_words, W
                     for h in range(HALVES_1):
                         repeat_on_all_partitions(h, minus_g1_all[:, h, :], -1.0, "p (q t) -> p t q", False)
                         repeat_on_all_partitions(HALVES_1 + h, b1_all[:, h, :], 1.0, "p (q t) -> p t q", False)
+                    repeat_on_all_partitions(2 * HALVES_1, minus_g2_all[:], -1.0, "p (t q) -> p t q", True)
+                    repeat_on_all_partitions(2 * HALVES_1 + 1, b2_all[:], 1.0, "p (t q) -> p t q", True)
                 w1_chunks.append(load_w1_chunk(len(w1_chunks)))
                 if waiting is not None:
                     quantise_x_chunk(*waiting)
@@ -171,11 +173,12 @@ def tile_autoencoder_pa_k_kernel(tc, x, W1_words, W1_scales, g1, b1, W2_words, W
             [sums.tile([P, N_PASS], F32, name="u1_%d%d" % (m, h), tag="sum%d%d" % (m, h)) for h in range(HALVES_1)]
             for m in range(TOKEN_TILES)
         ]
-        for j in range(W_CHUNKS):
+
+        def passes_of_chunk(j, token_tiles):
             for i in range(W_CHUNK_PASSES):
                 g = j * W_CHUNK_PASSES + i
                 offset = 4 * (g % PLANES_PER_TILE)
-                for m in range(TOKEN_TILES):
+                for m in token_tiles:
                     for h in range(HALVES_1):
                         features = slice(h * N_PASS, (h + 1) * N_PASS)
                         nc.tensor.matmul_mx(
@@ -187,48 +190,56 @@ def tile_autoencoder_pa_k_kernel(tc, x, W1_words, W1_scales, g1, b1, W2_words, W
                             start=(g == 0),
                             stop=(g == PASSES_1 - 1),
                         )
+
+        for j in range(W_CHUNKS - TILE_BY_TILE_CHUNKS):
+            passes_of_chunk(j, range(TOKEN_TILES))
             if len(w1_chunks) < W_CHUNKS:
                 w1_chunks.append(load_w1_chunk(len(w1_chunks)))
+        for m in range(TOKEN_TILES):
+            for j in range(W_CHUNKS - TILE_BY_TILE_CHUNKS, W_CHUNKS):
+                passes_of_chunk(j, [m])
         nc.sync.dma_start(out=w2_words[:].bitcast(I32), in_=W2_words.rearrange("g p n t -> p g (n t)").bitcast(I32))
 
         with tc.tile_pool(name="tail", bufs=1) as tail:
 
-            def row_statistics(label, rows_of_banks):
-                partials = []
-                for m, banks in enumerate(rows_of_banks):
-                    partial = tail.tile([P, len(banks), 6], F32, name="partial_%s%d" % (label, m))
-                    for i, bank in enumerate(banks):
-                        nc.vector.bn_stats(out=partial[:, i, :], in_=bank[:])
-                    partials.append(partial)
-                statistics = []
-                for m, partial in enumerate(partials):
-                    mean_var = tail.tile([P, 2], F32, name="mean_var_%s%d" % (label, m))
-                    nc.vector.bn_aggr(out=mean_var[:], in_=partial[:].rearrange("p b s -> p (b s)"))
-                    rstd = tail.tile([P, 1], F32, name="rstd_%s%d" % (label, m))
-                    nc.scalar.activation(
-                        out=rstd[:], in_=mean_var[:, 1:2], func=ACT.Abs_reciprocal_sqrt, bias=eps_col[:]
-                    )
-                    statistics.append((mean_var[:, 0:1], rstd[:]))
-                return statistics
-
-            def norm_and_mish(pieces, after):
+            def norm_and_mish(layer, groups, after):
                 work = []
-                for first in range(0, len(pieces), PAIR):
-                    pair = pieces[first : first + PAIR]
-                    centred_pair = []
-                    for u, (mean, rstd), minus_gain, bias, result, m in pair:
-                        centred = tail.tile([P, PACK, P], F32, name="centred", bufs=PAIR)
-                        nc.vector.scalar_tensor_tensor(
-                            out=centred[:], in0=u, scalar=mean, in1=minus_gain, op0=ALU.subtract, op1=ALU.mult
-                        )
-                        centred_pair.append(centred)
-                    for centred, (u, (mean, rstd), minus_gain, bias, result, m) in zip(centred_pair, pair):
+                for group in groups:
+                    partials = []
+                    for m, banks, pieces in group:
+                        partial = tail.tile([P, len(banks), 6], F32, name="partial_%d%d" % (layer, m))
+                        for i, bank in enumerate(banks):
+                            nc.vector.bn_stats(out=partial[:, i, :], in_=bank[:])
+                        partials.append(partial)
+                    statistics = []
+                    for partial, (m, banks, pieces) in zip(partials, group):
+                        mean_var = tail.tile([P, 2], F32, name="mean_var_%d%d" % (layer, m))
+                        nc.vector.bn_aggr(out=mean_var[:], in_=partial[:].rearrange("p b s -> p (b s)"))
+                        var_eps = tail.tile([P, 1], F32, name="var_eps_%d%d" % (layer, m))
+                        nc.vector.tensor_scalar_add(out=var_eps[:], in0=mean_var[:, 1:2], scalar1=EPS)
+                        rstd = tail.tile([P, 1], F32, name="rstd_%d%d" % (layer, m))
+                        nc.gpsimd.tensor_tensor(out=rstd[:], in0=var_eps[:], in1=minus_half[:], op=ALU.pow)
+                        statistics.append((mean_var, rstd))
+                    started = []
+                    for (mean_var, rstd), (m, banks, pieces) in zip(statistics, group):
+                        for u, minus_gain, bias, result in pieces:
+                            centred = tail.tile([P, PACK, P], F32, name="centred", bufs=2)
+                            nc.vector.scalar_tensor_tensor(
+                                out=centred[:],
+                                in0=u,
+                                scalar=mean_var[:, 0:1],
+                                in1=minus_gain,
+                                op0=ALU.subtract,
+                                op1=ALU.mult,
+                            )
+                            started.append((centred, rstd, bias, result, m))
+                    for centred, rstd, bias, result, m in started:
                         minus_v = tail.tile([P, N_PASS], F32, name="minus_v", bufs=4)
                         gate = tail.tile([P, N_PASS], F32, name="gate", bufs=4)
                         nc.vector.scalar_tensor_tensor(
                             out=minus_v[:],
                             in0=centred[:].rearrange("p t q -> p (t q)"),
-                            scalar=rstd,
+                            scalar=rstd[:],
                             in1=bias,
                             op0=ALU.mult,
                             op1=ALU.subtract,
@@ -254,21 +265,22 @@ def tile_autoencoder_pa_k_kernel(tc, x, W1_words, W1_scales, g1, b1, W2_words, W
                     )
                     after(i)
 
-            stats_1 = row_statistics("1", u1)
-            repeat_on_all_partitions(2 * HALVES_1, minus_g2_all[:], -1.0, "p (t q) -> p t q", True)
-            repeat_on_all_partitions(2 * HALVES_1 + 1, b2_all[:], 1.0, "p (t q) -> p t q", True)
             h1 = [tail.tile([P, PASSES_2, PACK, P], BF16, name="h1_%d" % m) for m in range(TOKEN_TILES)]
-            pieces_1 = [
+            tiles_1 = [
                 (
-                    u1[m][g][:].rearrange("p (q t) -> p t q", t=PACK),
-                    stats_1[m],
-                    minus_g1_all[:, g, :].rearrange("p (t q) -> p t q", t=PACK),
-                    b1_all[:, g, :],
-                    h1[m][:, g, :, :].rearrange("p t q -> p (t q)"),
                     m,
+                    u1[m],
+                    [
+                        (
+                            u1[m][g][:].rearrange("p (q t) -> p t q", t=PACK),
+                            minus_g1_all[:, g, :].rearrange("p (t q) -> p t q", t=PACK),
+                            b1_all[:, g, :],
+                            h1[m][:, g, :, :].rearrange("p t q -> p (t q)"),
+                        )
+                        for g in range(PASSES_2)
+                    ],
                 )
                 for m in range(TOKEN_TILES)
-                for g in range(PASSES_2)
             ]
             turned_h = []
 
@@ -279,7 +291,7 @@ def tile_autoencoder_pa_k_kernel(tc, x, W1_words, W1_scales, g1, b1, W2_words, W
                     nc.tensor.transpose(turned[:, t, :], h1[m][:, g, t, :], ident_bf16[:])
                 turned_h.append(turned)
 
-            norm_and_mish(pieces_1, transpose_h1)
+            norm_and_mish(1, [[token_tile] for token_tile in tiles_1], transpose_h1)
 
             grouped_h = [
                 tail.tile([P, PASSES_2, P, PACK], BF16, name="grouped_h%d" % m, align_bytes=64)
@@ -288,36 +300,38 @@ def tile_autoencoder_pa_k_kernel(tc, x, W1_words, W1_scales, g1, b1, W2_words, W
             for i, turned in enumerate(turned_h):
                 m, g = divmod(i, PASSES_2)
                 empty_bank(i, grouped_h[m][:, g, :, :], turned[:].rearrange("p t r -> p r t"))
-            u2 = []
+            u2 = [sums.tile([P, D_OUT], F32, name="u2_%d" % m, tag="sum%d0" % m) for m in range(TOKEN_TILES)]
             for m in range(TOKEN_TILES):
-                nc.vector.quantize_mx(
-                    out=h_codes[:, m, :].bitcast(FP8X4),
-                    scales=h_scales[:, m, :],
-                    in_=grouped_h[m][:].rearrange("p g r t -> p (g r t)"),
-                )
-                u2_m = sums.tile([P, D_OUT], F32, name="u2_%d" % m, tag="sum%d0" % m)
                 for g in range(PASSES_2):
+                    tokens = slice(g * P, (g + 1) * P)
+                    nc.vector.quantize_mx(
+                        out=h_codes[:, m, tokens].bitcast(FP8X4),
+                        scales=h_scales[:, m, tokens],
+                        in_=grouped_h[m][:, g, :, :].rearrange("p r t -> p (r t)"),
+                    )
                     nc.tensor.matmul_mx(
-                        out=u2_m[:],
-                        lhsT=h_codes[:, m, g * P : (g + 1) * P].bitcast(FP8X4),
-                        lhsT_scale=h_scales[:, m, g * P : (g + 1) * P],
+                        out=u2[m][:],
+                        lhsT=h_codes[:, m, tokens].bitcast(FP8X4),
+                        lhsT_scale=h_scales[:, m, tokens],
                         rhs=w2_words[:, g, :].bitcast(FP8X4),
                         rhs_scale=w2_planes[4 * g : P, :],
                         start=(g == 0),
                         stop=(g == PASSES_2 - 1),
                     )
-                u2.append(u2_m)
 
-            stats_2 = row_statistics("2", [[u2_m] for u2_m in u2])
             mish_2 = [tail.tile([P, D_OUT], F32, name="mish_2_%d" % m) for m in range(TOKEN_TILES)]
-            pieces_2 = [
+            tiles_2 = [
                 (
-                    u2[m][:].rearrange("p (t q) -> p t q", t=PACK),
-                    stats_2[m],
-                    minus_g2_all[:].rearrange("p (t q) -> p t q", t=PACK),
-                    b2_all[:],
-                    mish_2[m][:],
                     m,
+                    [u2[m]],
+                    [
+                        (
+                            u2[m][:].rearrange("p (t q) -> p t q", t=PACK),
+                            minus_g2_all[:].rearrange("p (t q) -> p t q", t=PACK),
+                            b2_all[:],
+                            mish_2[m][:],
+                        )
+                    ],
                 )
                 for m in range(TOKEN_TILES)
             ]
@@ -325,4 +339,4 @@ def tile_autoencoder_pa_k_kernel(tc, x, W1_words, W1_scales, g1, b1, W2_words, W
             def store_result(m):
                 nc.sync.dma_start(out=out[m * P : (m + 1) * P, :], in_=mish_2[m][:])
 
-            norm_and_mish(pieces_2, store_result)
+            norm_and_mish(2, [tiles_2], store_result)

@@ -55,9 +55,10 @@ def tile_autoencoder_pa_k_kernel(tc, x, W1_words, W1_scales, g1, b1, W2_words, W
         minus_half = keep.tile([P, 1], F32, name="minus_half")
         two_col = keep.tile([P, 1], F32, name="two_col")
         table_warm = keep.tile([P, 1], F32, name="table_warm")
+        make_identity(nc, ident_f32[:])
+        make_identity(nc, ident_bf16[:])
         nc.gpsimd.memset(minus_half[:], -0.5)
         nc.gpsimd.memset(two_col[:], 2.0)
-        make_identity(nc, ident_f32[:])
 
         x_codes = keep.tile([P, TOKEN_TILES, PASSES_1 * P], U32, name="x_codes", align_bytes=64)
         x_scales = keep.tile([P, TOKEN_TILES, PASSES_1 * P], U8, name="x_scales", align_bytes=64)
@@ -71,79 +72,124 @@ def tile_autoencoder_pa_k_kernel(tc, x, W1_words, W1_scales, g1, b1, W2_words, W
         minus_g2_all = keep.tile([P, D_OUT], F32, name="minus_g2_all")
         b2_all = keep.tile([P, D_OUT], F32, name="b2_all")
 
-        nc.vector.memset(w1_planes[:].bitcast(I32), 0)
-        nc.vector.memset(w2_planes[:].bitcast(I32), 0)
-        for s in range(PASSES_1 // PLANES_PER_TILE):
+        rows = keep.tile([P, P], BF16, name="rows", align_bytes=64)
+        nc.vector.memset(rows[:].bitcast(I32), 0)
+        first = 0
+        for vector in (g1, b1, g2, b2):
+            count = vector.shape[0] // P
+            nc.scalar.dma_start(out=rows[first : first + count, :], in_=vector.rearrange("(r n) -> r n", n=P))
+            first += count
+
+        def load_scales(s, queue, view):
             for quadrant in range(QUADRANTS):
-                nc.gpsimd.dma_start(
-                    out=w1_planes[32 * quadrant : 32 * quadrant + 16, s, :].bitcast(F32),
+                queue.dma_start(
+                    out=w1_planes[32 * quadrant : 32 * quadrant + 16, s, :].bitcast(view),
                     in_=W1_scales[
                         PLANES_PER_TILE * s : PLANES_PER_TILE * (s + 1), 4 * quadrant : 4 * quadrant + 4, :
-                    ].bitcast(F32),
+                    ].bitcast(view),
                 )
+
+        for s in range(PASSES_1 // PLANES_PER_TILE):
+            nc.vector.memset(w1_planes[:, s, :].bitcast(I32), 0)
+            if s > 0:
+                load_scales(s, nc.gpsimd, F32)
+        nc.vector.memset(w2_planes[:].bitcast(I32), 0)
         for quadrant in range(QUADRANTS):
             nc.gpsimd.dma_start(
                 out=w2_planes[32 * quadrant : 32 * quadrant + 4 * PASSES_2, :].bitcast(F32),
                 in_=W2_scales[:, 4 * quadrant : 4 * quadrant + 4, :].bitcast(F32),
             )
-        make_identity(nc, ident_bf16[:])
+        nc.scalar.activation(out=table_warm[:], in_=two_col[:], func=ACT.Exp)
 
-        def load_w1_chunk(j):
-            chunk = stream.tile([P, W_CHUNK_PASSES, D_HID], U32, name="w1_chunk", tag="stream", align_bytes=64)
-            for i in range(W_CHUNK_PASSES):
-                nc.sync.dma_start(
-                    out=chunk[:, i, :].bitcast(I32),
-                    in_=W1_words[j * W_CHUNK_PASSES + i].rearrange("p n t -> p (n t)").bitcast(I32),
+        order = [("x", 0, 0), ("x", 1, 0)]
+        w_per_stretch = X_CHUNK_PASSES // W_CHUNK_PASSES
+        for n in range(X_CHUNKS_PER_TILE):
+            for i in range(w_per_stretch):
+                order.append(("w", n * w_per_stretch + i))
+                if i % 2 == 0 and n + 1 < X_CHUNKS_PER_TILE:
+                    order.append(("x", i // 2, n + 1))
+        loaded = {}
+
+        def load_next():
+            if len(loaded) == len(order):
+                return
+            item = order[len(loaded)]
+            if item[0] == "x":
+                m, part = item[1], item[2]
+                buffer = stream.tile([P, X_CHUNK_K], BF16, name="x_chunk", tag="stream", align_bytes=64)
+                pieces = 4 if len(loaded) == 0 else 1
+                width = X_CHUNK_K // pieces
+                for i in range(pieces):
+                    nc.sync.dma_start(
+                        out=buffer[:, i * width : (i + 1) * width],
+                        in_=x[m * P : (m + 1) * P, part * X_CHUNK_K + i * width : part * X_CHUNK_K + (i + 1) * width],
+                    )
+            else:
+                buffer = stream.tile([P, W_CHUNK_PASSES, D_HID], U32, name="w1_chunk", tag="stream", align_bytes=64)
+                for i in range(W_CHUNK_PASSES):
+                    nc.sync.dma_start(
+                        out=buffer[:, i, :].bitcast(I32),
+                        in_=W1_words[item[1] * W_CHUNK_PASSES + i].rearrange("p n t -> p (n t)").bitcast(I32),
+                    )
+            loaded[item] = buffer
+
+        u1 = [
+            [sums.tile([P, N_PASS], F32, name="u1_%d%d" % (m, h), tag="sum%d%d" % (m, h)) for h in range(HALVES_1)]
+            for m in range(TOKEN_TILES)
+        ]
+
+        def passes_of_chunk(j, token_tiles):
+            for m in token_tiles:
+                for i in range(W_CHUNK_PASSES):
+                    g = j * W_CHUNK_PASSES + i
+                    offset = 4 * (g % PLANES_PER_TILE)
+                    for h in range(HALVES_1):
+                        features = slice(h * N_PASS, (h + 1) * N_PASS)
+                        nc.tensor.matmul_mx(
+                            out=u1[m][h][:],
+                            lhsT=x_codes[:, m, g * P : (g + 1) * P].bitcast(FP8X4),
+                            lhsT_scale=x_scales[:, m, g * P : (g + 1) * P],
+                            rhs=loaded[("w", j)][:, i, features].bitcast(FP8X4),
+                            rhs_scale=w1_planes[offset:P, g // PLANES_PER_TILE, features],
+                            start=(g == 0),
+                            stop=(g == PASSES_1 - 1),
+                        )
+
+        def repeat_on_all_partitions(block, target, sign, pattern, on_scalar):
+            repeated = turn.tile([P, N_PASS], F32, name="repeated", tag="turn")
+            for i in range(N_PASS // P):
+                row = block * (N_PASS // P) + i
+                nc.tensor.matmul(
+                    out=repeated[:, i * P : (i + 1) * P],
+                    lhsT=ident_bf16[:, row : row + 1].to_broadcast([P, P]),
+                    rhs=rows[:],
+                    start=True,
+                    stop=True,
                 )
-            return chunk
+            dst = target.rearrange("p (t q) -> p t q", t=PACK)
+            src = repeated[:].rearrange(pattern, t=PACK)
+            if on_scalar:
+                nc.scalar.mul(out=dst, in_=src, mul=sign)
+            else:
+                nc.vector.tensor_scalar_mul(out=dst, in0=src, scalar1=sign)
 
         with tc.tile_pool(name="stage", bufs=3) as stage:
-            rows = keep.tile([P, 2 * D_HID + 2 * D_OUT], BF16, name="rows")
-            ones = keep.tile([P, P], BF16, name="ones")
-            nc.vector.memset(rows[:].bitcast(I32), 0)
-            nc.vector.memset(ones[:], 1.0)
-            first = 0
-            for vector in (g1, b1, g2, b2):
-                width = vector.shape[0]
-                nc.scalar.dma_start(out=rows[0:1, first : first + width], in_=vector.unsqueeze(0))
-                first += width
-            nc.scalar.activation(out=table_warm[:], in_=two_col[:], func=ACT.Exp)
 
-            x_chunks = []
-            for c in range(X_CHUNKS):
-                m, part = divmod(c, X_CHUNKS_PER_TILE)
-                x_chunk = stream.tile([P, X_CHUNK_K], BF16, name="x_chunk", tag="stream", align_bytes=64)
-                nc.sync.dma_start(
-                    out=x_chunk[:], in_=x[m * P : (m + 1) * P, part * X_CHUNK_K : (part + 1) * X_CHUNK_K]
-                )
-                x_chunks.append(x_chunk)
-
-            w1_chunks = [load_w1_chunk(j) for j in range(STREAM_BUFS - X_CHUNKS)]
-
-            def repeat_on_all_partitions(block, target, sign, order, on_scalar):
-                repeated = turn.tile([P, N_PASS], F32, name="repeated", tag="turn")
-                nc.tensor.matmul(
-                    out=repeated[:], lhsT=ones[:], rhs=rows[:, block * N_PASS : (block + 1) * N_PASS], start=True, stop=True
-                )
-                dst = target.rearrange("p (t q) -> p t q", t=PACK)
-                src = repeated[:].rearrange(order, t=PACK)
-                if on_scalar:
-                    nc.scalar.mul(out=dst, in_=src, mul=sign)
-                else:
-                    nc.vector.tensor_scalar_mul(out=dst, in0=src, scalar1=sign)
-
-            def quantise_x_chunk(c, grouped):
-                m, part = divmod(c, X_CHUNKS_PER_TILE)
-                columns = slice(part * X_CHUNK_PASSES * P, (part + 1) * X_CHUNK_PASSES * P)
-                nc.vector.quantize_mx(
-                    out=x_codes[:, m, columns].bitcast(FP8X4), scales=x_scales[:, m, columns], in_=grouped[:]
-                )
-
-            waiting = None
-            for c in range(X_CHUNKS):
-                words = x_chunks[c][:].bitcast(F32)
+            def transpose_and_quantise(m, part):
+                words = loaded[("x", m, part)][:].bitcast(F32)
                 grouped = stage.tile([P, X_CHUNK_K], BF16, name="grouped", align_bytes=64)
                 grouped_words = grouped[:].bitcast(F32).rearrange("p (g r u) -> p g r u", g=X_CHUNK_PASSES, u=2)
+
+                def quantise(half):
+                    width = X_CHUNK_K // 2
+                    first_column = part * X_CHUNK_PASSES * P + half * (width // PACK)
+                    columns = slice(first_column, first_column + width // PACK)
+                    nc.vector.quantize_mx(
+                        out=x_codes[:, m, columns].bitcast(FP8X4),
+                        scales=x_scales[:, m, columns],
+                        in_=grouped[:, half * width : (half + 1) * width],
+                    )
+
                 for bank in range(X_CHUNK_PASSES // BANK_PASSES):
                     turned = turn.tile([P, BANK_PASSES, 2, P], F32, name="turned", tag="turn")
                     for i in range(BANK_PASSES):
@@ -157,44 +203,27 @@ def tile_autoencoder_pa_k_kernel(tc, x, W1_words, W1_scales, g1, b1, W2_words, W
                         grouped_words[:, bank * BANK_PASSES : (bank + 1) * BANK_PASSES, :, :],
                         turned[:].rearrange("p g u r -> p g r u"),
                     )
-                if c == 0:
+                    if bank == 2:
+                        quantise(0)
+                quantise(1)
+
+            for i in range(STREAM_BUFS):
+                load_next()
+                if i == 0:
+                    load_scales(0, nc.sync, I32)
+            for position, item in enumerate(order[: len(order) - TILE_BY_TILE_CHUNKS]):
+                if item[0] == "x":
+                    transpose_and_quantise(item[1], item[2])
+                else:
+                    passes_of_chunk(item[1], range(TOKEN_TILES))
+                load_next()
+                if position == 1:
                     for h in range(HALVES_1):
                         repeat_on_all_partitions(h, minus_g1_all[:, h, :], -1.0, "p (q t) -> p t q", False)
-                        repeat_on_all_partitions(HALVES_1 + h, b1_all[:, h, :], 1.0, "p (q t) -> p t q", False)
-                    repeat_on_all_partitions(2 * HALVES_1, minus_g2_all[:], -1.0, "p (t q) -> p t q", True)
+                        repeat_on_all_partitions(HALVES_1 + h, b1_all[:, h, :], 1.0, "p (q t) -> p t q", True)
+                    repeat_on_all_partitions(2 * HALVES_1, minus_g2_all[:], -1.0, "p (t q) -> p t q", False)
                     repeat_on_all_partitions(2 * HALVES_1 + 1, b2_all[:], 1.0, "p (t q) -> p t q", True)
-                w1_chunks.append(load_w1_chunk(len(w1_chunks)))
-                if waiting is not None:
-                    quantise_x_chunk(*waiting)
-                waiting = (c, grouped)
-            quantise_x_chunk(*waiting)
 
-        u1 = [
-            [sums.tile([P, N_PASS], F32, name="u1_%d%d" % (m, h), tag="sum%d%d" % (m, h)) for h in range(HALVES_1)]
-            for m in range(TOKEN_TILES)
-        ]
-
-        def passes_of_chunk(j, token_tiles):
-            for i in range(W_CHUNK_PASSES):
-                g = j * W_CHUNK_PASSES + i
-                offset = 4 * (g % PLANES_PER_TILE)
-                for m in token_tiles:
-                    for h in range(HALVES_1):
-                        features = slice(h * N_PASS, (h + 1) * N_PASS)
-                        nc.tensor.matmul_mx(
-                            out=u1[m][h][:],
-                            lhsT=x_codes[:, m, g * P : (g + 1) * P].bitcast(FP8X4),
-                            lhsT_scale=x_scales[:, m, g * P : (g + 1) * P],
-                            rhs=w1_chunks[j][:, i, features].bitcast(FP8X4),
-                            rhs_scale=w1_planes[offset:P, g // PLANES_PER_TILE, features],
-                            start=(g == 0),
-                            stop=(g == PASSES_1 - 1),
-                        )
-
-        for j in range(W_CHUNKS - TILE_BY_TILE_CHUNKS):
-            passes_of_chunk(j, range(TOKEN_TILES))
-            if len(w1_chunks) < W_CHUNKS:
-                w1_chunks.append(load_w1_chunk(len(w1_chunks)))
         for m in range(TOKEN_TILES):
             for j in range(W_CHUNKS - TILE_BY_TILE_CHUNKS, W_CHUNKS):
                 passes_of_chunk(j, [m])

@@ -54,11 +54,13 @@ def tile_autoencoder_pa_k_kernel(tc, x, W1_words, W1_scales, g1, b1, W2_words, W
         ident_bf16 = keep.tile([P, P], BF16, name="ident_bf16")
         minus_half = keep.tile([P, 1], F32, name="minus_half")
         two_col = keep.tile([P, 1], F32, name="two_col")
+        eps_col = keep.tile([P, 1], F32, name="eps_col")
         table_warm = keep.tile([P, 1], F32, name="table_warm")
         make_identity(nc, ident_f32[:])
         make_identity(nc, ident_bf16[:])
         nc.gpsimd.memset(minus_half[:], -0.5)
         nc.gpsimd.memset(two_col[:], 2.0)
+        nc.gpsimd.memset(eps_col[:], EPS)
 
         x_codes = keep.tile([P, TOKEN_TILES, PASSES_1 * P], U32, name="x_codes", align_bytes=64)
         x_scales = keep.tile([P, TOKEN_TILES, PASSES_1 * P], U8, name="x_scales", align_bytes=64)
@@ -74,11 +76,6 @@ def tile_autoencoder_pa_k_kernel(tc, x, W1_words, W1_scales, g1, b1, W2_words, W
 
         rows = keep.tile([P, P], BF16, name="rows", align_bytes=64)
         nc.vector.memset(rows[:].bitcast(I32), 0)
-        first = 0
-        for vector in (g1, b1, g2, b2):
-            count = vector.shape[0] // P
-            nc.scalar.dma_start(out=rows[first : first + count, :], in_=vector.rearrange("(r n) -> r n", n=P))
-            first += count
 
         def load_scales(s, queue, view):
             for quadrant in range(QUADRANTS):
@@ -93,13 +90,19 @@ def tile_autoencoder_pa_k_kernel(tc, x, W1_words, W1_scales, g1, b1, W2_words, W
             nc.vector.memset(w1_planes[:, s, :].bitcast(I32), 0)
             if s > 0:
                 load_scales(s, nc.gpsimd, F32)
+            if s == 1:
+                first = 0
+                for vector in (g1, b1, g2, b2):
+                    count = vector.shape[0] // P
+                    nc.gpsimd.dma_start(out=rows[first : first + count, :], in_=vector.rearrange("(r n) -> r n", n=P))
+                    first += count
         nc.vector.memset(w2_planes[:].bitcast(I32), 0)
         for quadrant in range(QUADRANTS):
             nc.gpsimd.dma_start(
                 out=w2_planes[32 * quadrant : 32 * quadrant + 4 * PASSES_2, :].bitcast(F32),
                 in_=W2_scales[:, 4 * quadrant : 4 * quadrant + 4, :].bitcast(F32),
             )
-        nc.scalar.activation(out=table_warm[:], in_=two_col[:], func=ACT.Exp)
+        nc.scalar.activation(out=table_warm[:], in_=two_col[:], func=ACT.Abs_reciprocal_sqrt)
 
         order = [("x", 0, 0), ("x", 1, 0)]
         w_per_stretch = X_CHUNK_PASSES // W_CHUNK_PASSES
@@ -117,7 +120,7 @@ def tile_autoencoder_pa_k_kernel(tc, x, W1_words, W1_scales, g1, b1, W2_words, W
             if item[0] == "x":
                 m, part = item[1], item[2]
                 buffer = stream.tile([P, X_CHUNK_K], BF16, name="x_chunk", tag="stream", align_bytes=64)
-                pieces = 4 if len(loaded) == 0 else 1
+                pieces = 2 if len(loaded) == 0 else 1
                 width = X_CHUNK_K // pieces
                 for i in range(pieces):
                     nc.sync.dma_start(
@@ -209,7 +212,7 @@ def tile_autoencoder_pa_k_kernel(tc, x, W1_words, W1_scales, g1, b1, W2_words, W
 
             for i in range(STREAM_BUFS):
                 load_next()
-                if i == 0:
+                if i == 1:
                     load_scales(0, nc.sync, I32)
             for position, item in enumerate(order[: len(order) - TILE_BY_TILE_CHUNKS]):
                 if item[0] == "x":
@@ -217,7 +220,7 @@ def tile_autoencoder_pa_k_kernel(tc, x, W1_words, W1_scales, g1, b1, W2_words, W
                 else:
                     passes_of_chunk(item[1], range(TOKEN_TILES))
                 load_next()
-                if position == 1:
+                if item == ("w", 2):
                     for h in range(HALVES_1):
                         repeat_on_all_partitions(h, minus_g1_all[:, h, :], -1.0, "p (q t) -> p t q", False)
                         repeat_on_all_partitions(HALVES_1 + h, b1_all[:, h, :], 1.0, "p (q t) -> p t q", True)
@@ -231,96 +234,122 @@ def tile_autoencoder_pa_k_kernel(tc, x, W1_words, W1_scales, g1, b1, W2_words, W
 
         with tc.tile_pool(name="tail", bufs=1) as tail:
 
-            def norm_and_mish(layer, groups, after):
-                work = []
-                for group in groups:
-                    partials = []
-                    for m, banks, pieces in group:
-                        partial = tail.tile([P, len(banks), 6], F32, name="partial_%d%d" % (layer, m))
-                        for i, bank in enumerate(banks):
-                            nc.vector.bn_stats(out=partial[:, i, :], in_=bank[:])
-                        partials.append(partial)
-                    statistics = []
-                    for partial, (m, banks, pieces) in zip(partials, group):
-                        mean_var = tail.tile([P, 2], F32, name="mean_var_%d%d" % (layer, m))
-                        nc.vector.bn_aggr(out=mean_var[:], in_=partial[:].rearrange("p b s -> p (b s)"))
-                        var_eps = tail.tile([P, 1], F32, name="var_eps_%d%d" % (layer, m))
-                        nc.vector.tensor_scalar_add(out=var_eps[:], in0=mean_var[:, 1:2], scalar1=EPS)
-                        rstd = tail.tile([P, 1], F32, name="rstd_%d%d" % (layer, m))
-                        nc.gpsimd.tensor_tensor(out=rstd[:], in0=var_eps[:], in1=minus_half[:], op=ALU.pow)
-                        statistics.append((mean_var, rstd))
-                    started = []
-                    for (mean_var, rstd), (m, banks, pieces) in zip(statistics, group):
-                        for u, minus_gain, bias, result in pieces:
-                            centred = tail.tile([P, PACK, P], F32, name="centred", bufs=2)
-                            nc.vector.scalar_tensor_tensor(
-                                out=centred[:],
-                                in0=u,
-                                scalar=mean_var[:, 0:1],
-                                in1=minus_gain,
-                                op0=ALU.subtract,
-                                op1=ALU.mult,
-                            )
-                            started.append((centred, rstd, bias, result, m))
-                    for centred, rstd, bias, result, m in started:
-                        minus_v = tail.tile([P, N_PASS], F32, name="minus_v", bufs=4)
-                        gate = tail.tile([P, N_PASS], F32, name="gate", bufs=4)
-                        nc.vector.scalar_tensor_tensor(
-                            out=minus_v[:],
-                            in0=centred[:].rearrange("p t q -> p (t q)"),
-                            scalar=rstd[:],
-                            in1=bias,
-                            op0=ALU.mult,
-                            op1=ALU.subtract,
-                        )
-                        nc.scalar.activation(out=gate[:], in_=minus_v[:], func=ACT.Exp, scale=-1.0)
-                        work.append((minus_v, gate, result, m))
-                for minus_v, gate, result, m in work:
-                    nc.vector.scalar_tensor_tensor(
-                        out=gate[:], in0=gate[:], scalar=2.0, in1=gate[:], op0=ALU.add, op1=ALU.mult
-                    )
-                for minus_v, gate, result, m in work:
-                    nc.scalar.activation(out=gate[:], in_=gate[:], func=ACT.Abs_reciprocal_sqrt, bias=two_col[:])
-                for minus_v, gate, result, m in work:
-                    if m == 0:
-                        nc.vector.scalar_tensor_tensor(
-                            out=gate[:], in0=gate[:], scalar=2.0, in1=gate[:], op0=ALU.mult, op1=ALU.mult
-                        )
-                    else:
-                        nc.scalar.activation(out=gate[:], in_=gate[:], func=ACT.Square, scale=SQRT_2)
-                for i, (minus_v, gate, result, m) in enumerate(work):
-                    nc.vector.scalar_tensor_tensor(
-                        out=result, in0=gate[:], scalar=1.0, in1=minus_v[:], op0=ALU.subtract, op1=ALU.mult
-                    )
-                    after(i)
+            def statistics(name, banks):
+                partial = tail.tile([P, len(banks), 6], F32, name="partial_" + name)
+                for i, bank in enumerate(banks):
+                    nc.vector.bn_stats(out=partial[:, i, :], in_=bank[:])
+                mean_var = tail.tile([P, 2], F32, name="mean_var_" + name)
+                nc.vector.bn_aggr(out=mean_var[:], in_=partial[:].rearrange("p b s -> p (b s)"))
+                return mean_var
+
+            def rstd_on_scalar(name, mean_var):
+                rstd = tail.tile([P, 1], F32, name="rstd_" + name)
+                nc.scalar.activation(out=rstd[:], in_=mean_var[:, 1:2], func=ACT.Abs_reciprocal_sqrt, bias=eps_col[:])
+                return rstd
+
+            def rstd_on_gpsimd(name, mean_var):
+                var_eps = tail.tile([P, 1], F32, name="var_eps_" + name)
+                nc.vector.tensor_scalar_add(out=var_eps[:], in0=mean_var[:, 1:2], scalar1=EPS)
+                rstd = tail.tile([P, 1], F32, name="rstd_" + name)
+                nc.gpsimd.tensor_tensor(out=rstd[:], in0=var_eps[:], in1=minus_half[:], op=ALU.pow)
+                return rstd
+
+            def centre(piece, mean_var):
+                centred = tail.tile([P, PACK, P], F32, name="centred", bufs=2)
+                nc.vector.scalar_tensor_tensor(
+                    out=centred[:],
+                    in0=piece["u"],
+                    scalar=mean_var[:, 0:1],
+                    in1=piece["minus_gain"],
+                    op0=ALU.subtract,
+                    op1=ALU.mult,
+                )
+                piece["centred"] = centred
+
+            def affine_and_exp(piece, rstd):
+                minus_v = tail.tile([P, N_PASS], F32, name="minus_v", bufs=4)
+                gate = tail.tile([P, N_PASS], F32, name="gate", bufs=4)
+                nc.vector.scalar_tensor_tensor(
+                    out=minus_v[:],
+                    in0=piece["centred"][:].rearrange("p t q -> p (t q)"),
+                    scalar=rstd[:],
+                    in1=piece["bias"],
+                    op0=ALU.mult,
+                    op1=ALU.subtract,
+                )
+                nc.scalar.activation(out=gate[:], in_=minus_v[:], func=ACT.Exp, scale=-1.0)
+                piece["minus_v"] = minus_v
+                piece["gate"] = gate
+
+            ALL = slice(0, N_PASS)
+
+            def form_n(piece, part=ALL):
+                gate = piece["gate"][:, part]
+                nc.vector.scalar_tensor_tensor(out=gate, in0=gate, scalar=2.0, in1=gate, op0=ALU.add, op1=ALU.mult)
+
+            def root(piece, part=ALL):
+                gate = piece["gate"][:, part]
+                nc.scalar.activation(out=gate, in_=gate, func=ACT.Abs_reciprocal_sqrt, bias=two_col[:])
+
+            def square_on_vector(piece, part=ALL):
+                gate = piece["gate"][:, part]
+                nc.vector.scalar_tensor_tensor(out=gate, in0=gate, scalar=2.0, in1=gate, op0=ALU.mult, op1=ALU.mult)
+
+            def square_on_scalar(piece, part=ALL):
+                gate = piece["gate"][:, part]
+                nc.scalar.activation(out=gate, in_=gate, func=ACT.Square, scale=SQRT_2)
+
+            def finish(piece, part=ALL):
+                nc.vector.scalar_tensor_tensor(
+                    out=piece["result"][:, part],
+                    in0=piece["gate"][:, part],
+                    scalar=1.0,
+                    in1=piece["minus_v"][:, part],
+                    op0=ALU.subtract,
+                    op1=ALU.mult,
+                )
 
             h1 = [tail.tile([P, PASSES_2, PACK, P], BF16, name="h1_%d" % m) for m in range(TOKEN_TILES)]
-            tiles_1 = [
-                (
-                    m,
-                    u1[m],
-                    [
-                        (
-                            u1[m][g][:].rearrange("p (q t) -> p t q", t=PACK),
-                            minus_g1_all[:, g, :].rearrange("p (t q) -> p t q", t=PACK),
-                            b1_all[:, g, :],
-                            h1[m][:, g, :, :].rearrange("p t q -> p (t q)"),
-                        )
-                        for g in range(PASSES_2)
-                    ],
-                )
+            pieces_1 = [
+                [
+                    {
+                        "u": u1[m][g][:].rearrange("p (q t) -> p t q", t=PACK),
+                        "minus_gain": minus_g1_all[:, g, :].rearrange("p (t q) -> p t q", t=PACK),
+                        "bias": b1_all[:, g, :],
+                        "result": h1[m][:, g, :, :].rearrange("p t q -> p (t q)"),
+                    }
+                    for g in range(PASSES_2)
+                ]
                 for m in range(TOKEN_TILES)
             ]
+            mean_var = statistics("10", u1[0])
+            rstd = rstd_on_scalar("10", mean_var)
+            for piece in pieces_1[0]:
+                centre(piece, mean_var)
+            for piece in pieces_1[0]:
+                affine_and_exp(piece, rstd)
+            mean_var = statistics("11", u1[1])
+            rstd = rstd_on_gpsimd("11", mean_var)
+            for piece in pieces_1[1]:
+                centre(piece, mean_var)
+            for piece in pieces_1[1]:
+                affine_and_exp(piece, rstd)
+            for piece in pieces_1[0] + pieces_1[1]:
+                form_n(piece)
+            for piece in pieces_1[0] + pieces_1[1]:
+                root(piece)
+            for piece in pieces_1[0]:
+                square_on_vector(piece)
+            for piece in pieces_1[1]:
+                square_on_scalar(piece)
             turned_h = []
-
-            def transpose_h1(i):
-                m, g = divmod(i, PASSES_2)
-                turned = turn.tile([P, PACK, P], BF16, name="turned_h", tag="turn")
-                for t in range(PACK):
-                    nc.tensor.transpose(turned[:, t, :], h1[m][:, g, t, :], ident_bf16[:])
-                turned_h.append(turned)
-
-            norm_and_mish(1, [[token_tile] for token_tile in tiles_1], transpose_h1)
+            for m in range(TOKEN_TILES):
+                for g in range(PASSES_2):
+                    finish(pieces_1[m][g])
+                    turned = turn.tile([P, PACK, P], BF16, name="turned_h", tag="turn")
+                    for t in range(PACK):
+                        nc.tensor.transpose(turned[:, t, :], h1[m][:, g, t, :], ident_bf16[:])
+                    turned_h.append(turned)
 
             grouped_h = [
                 tail.tile([P, PASSES_2, P, PACK], BF16, name="grouped_h%d" % m, align_bytes=64)
@@ -349,23 +378,32 @@ def tile_autoencoder_pa_k_kernel(tc, x, W1_words, W1_scales, g1, b1, W2_words, W
                     )
 
             mish_2 = [tail.tile([P, D_OUT], F32, name="mish_2_%d" % m) for m in range(TOKEN_TILES)]
-            tiles_2 = [
-                (
-                    m,
-                    [u2[m]],
-                    [
-                        (
-                            u2[m][:].rearrange("p (t q) -> p t q", t=PACK),
-                            minus_g2_all[:].rearrange("p (t q) -> p t q", t=PACK),
-                            b2_all[:],
-                            mish_2[m][:],
-                        )
-                    ],
-                )
+            pieces_2 = [
+                {
+                    "u": u2[m][:].rearrange("p (t q) -> p t q", t=PACK),
+                    "minus_gain": minus_g2_all[:].rearrange("p (t q) -> p t q", t=PACK),
+                    "bias": b2_all[:],
+                    "result": mish_2[m][:],
+                }
                 for m in range(TOKEN_TILES)
             ]
-
-            def store_result(m):
-                nc.sync.dma_start(out=out[m * P : (m + 1) * P, :], in_=mish_2[m][:])
-
-            norm_and_mish(2, [tiles_2], store_result)
+            mean_vars = [statistics("2%d" % m, [u2[m]]) for m in range(TOKEN_TILES)]
+            rstds = [rstd_on_scalar("2%d" % m, mean_vars[m]) for m in range(TOKEN_TILES)]
+            for m, piece in enumerate(pieces_2):
+                centre(piece, mean_vars[m])
+            for m, piece in enumerate(pieces_2):
+                affine_and_exp(piece, rstds[m])
+            for piece in pieces_2:
+                form_n(piece)
+            halves = [slice(0, N_PASS // 2), slice(N_PASS // 2, N_PASS)]
+            root(pieces_2[0])
+            for half in halves:
+                root(pieces_2[1], half)
+            square_on_vector(pieces_2[0])
+            square_on_vector(pieces_2[1], halves[0])
+            square_on_scalar(pieces_2[1], halves[1])
+            finish(pieces_2[0])
+            nc.sync.dma_start(out=out[0:P, :], in_=mish_2[0][:])
+            for half, queue in zip(halves, (nc.scalar, nc.sync)):
+                finish(pieces_2[1], half)
+                queue.dma_start(out=out[P : 2 * P, half], in_=mish_2[1][:, half])

import concourse.mybir as mybir
from concourse.masks import make_identity

F32 = mybir.dt.float32
BF16 = mybir.dt.bfloat16
I32 = mybir.dt.int32
U32 = mybir.dt.uint32
U8 = mybir.dt.uint8
FP8X4 = mybir.dt.float8_e4m3fn_x4
ALU = mybir.AluOpType
ACT = mybir.ActivationFunctionType

P = 128
PACK = 4
K_PASS = P * PACK
N_PASS = 512

TOKENS, D_IN, D_HID, D_OUT = 256, 16384, 1024, 512
EPS = 1e-5
FLOPS = 2 * TOKENS * D_IN * D_HID + 2 * TOKENS * D_HID * D_OUT

TOKEN_TILES = TOKENS // P
PASSES_1 = D_IN // K_PASS
PASSES_2 = D_HID // K_PASS
HALVES_1 = D_HID // N_PASS

X_CHUNK_K = 4096
X_CHUNK_PASSES = X_CHUNK_K // K_PASS
X_CHUNKS_PER_TILE = D_IN // X_CHUNK_K
X_CHUNKS = TOKEN_TILES * X_CHUNKS_PER_TILE
BANK_PASSES = 2
W_CHUNK_PASSES = 2
W_CHUNKS = PASSES_1 // W_CHUNK_PASSES
STREAM_BUFS = 14
PLANES_PER_TILE = 4
QUADRANTS = 4
TILE_BY_TILE_CHUNKS = 3
SQRT_2 = 2.0**0.5


def tile_autoencoder_pa_k_kernel(tc, x, W1_words, W1_scales, g1, b1, W2_words, W2_scales, g2, b2, out):
    nc = tc.nc

    def empty_bank(index, dst, src):
        if index % 4 == 2:
            nc.vector.tensor_copy(out=dst, in_=src)
        else:
            nc.scalar.copy(out=dst, in_=src)

    with tc.manual_schedule(), tc.tile_pool(name="keep", bufs=1) as keep, tc.tile_pool(
        name="stream", bufs=STREAM_BUFS
    ) as stream, tc.psum_pool(name="turn", bufs=4) as turn, tc.psum_pool(name="sums", bufs=1) as sums:
        ident_f32 = keep.tile([P, P], F32, name="ident_f32")
        ident_bf16 = keep.tile([P, P], BF16, name="ident_bf16")
        minus_half = keep.tile([P, 1], F32, name="minus_half")
        two_col = keep.tile([P, 1], F32, name="two_col")
        eps_col = keep.tile([P, 1], F32, name="eps_col")
        table_warm = keep.tile([P, 1], F32, name="table_warm")
        make_identity(nc, ident_f32[:])
        make_identity(nc, ident_bf16[:])
        nc.gpsimd.memset(minus_half[:], -0.5)
        nc.gpsimd.memset(two_col[:], 2.0)
        nc.gpsimd.memset(eps_col[:], EPS)

        x_codes = keep.tile([P, TOKEN_TILES, PASSES_1 * P], U32, name="x_codes", align_bytes=64)
        x_scales = keep.tile([P, TOKEN_TILES, PASSES_1 * P], U8, name="x_scales", align_bytes=64)
        w1_planes = keep.tile([P, PASSES_1 // PLANES_PER_TILE, D_HID], U8, name="w1_planes", align_bytes=64)
        w2_words = keep.tile([P, PASSES_2, D_OUT], U32, name="w2_words", align_bytes=64)
        w2_planes = keep.tile([P, D_OUT], U8, name="w2_planes", align_bytes=64)
        h_codes = keep.tile([P, TOKEN_TILES, PASSES_2 * P], U32, name="h_codes", align_bytes=64)
        h_scales = keep.tile([P, TOKEN_TILES, PASSES_2 * P], U8, name="h_scales", align_bytes=64)
        minus_g1_all = keep.tile([P, HALVES_1, N_PASS], F32, name="minus_g1_all")
        b1_all = keep.tile([P, HALVES_1, N_PASS], F32, name="b1_all")
        minus_g2_all = keep.tile([P, D_OUT], F32, name="minus_g2_all")
        b2_all = keep.tile([P, D_OUT], F32, name="b2_all")

        rows = keep.tile([P, P], BF16, name="rows", align_bytes=64)
        nc.vector.memset(rows[:].bitcast(I32), 0)

        def load_scales(s, queue, view):
            for quadrant in range(QUADRANTS):
                queue.dma_start(
                    out=w1_planes[32 * quadrant : 32 * quadrant + 16, s, :].bitcast(view),
                    in_=W1_scales[
                        PLANES_PER_TILE * s : PLANES_PER_TILE * (s + 1), 4 * quadrant : 4 * quadrant + 4, :
                    ].bitcast(view),
                )

        for s in range(PASSES_1 // PLANES_PER_TILE):
            nc.vector.memset(w1_planes[:, s, :].bitcast(I32), 0)
            if s > 0:
                load_scales(s, nc.gpsimd, F32)
            if s == 1:
                first = 0
                for vector in (g1, b1, g2, b2):
                    count = vector.shape[0] // P
                    nc.gpsimd.dma_start(out=rows[first : first + count, :], in_=vector.rearrange("(r n) -> r n", n=P))
                    first += count
        nc.vector.memset(w2_planes[:].bitcast(I32), 0)
        for quadrant in range(QUADRANTS):
            nc.gpsimd.dma_start(
                out=w2_planes[32 * quadrant : 32 * quadrant + 4 * PASSES_2, :].bitcast(F32),
                in_=W2_scales[:, 4 * quadrant : 4 * quadrant + 4, :].bitcast(F32),
            )
        nc.scalar.activation(out=table_warm[:], in_=two_col[:], func=ACT.Abs_reciprocal_sqrt)

        order = [("x", 0, 0), ("x", 1, 0)]
        w_per_stretch = X_CHUNK_PASSES // W_CHUNK_PASSES
        for n in range(X_CHUNKS_PER_TILE):
            for i in range(w_per_stretch):
                order.append(("w", n * w_per_stretch + i))
                if i % 2 == 0 and n + 1 < X_CHUNKS_PER_TILE:
                    order.append(("x", i // 2, n + 1))
        loaded = {}

        def load_next():
            if len(loaded) == len(order):
                return
            item = order[len(loaded)]
            if item[0] == "x":
                m, part = item[1], item[2]
                buffer = stream.tile([P, X_CHUNK_K], BF16, name="x_chunk", tag="stream", align_bytes=64)
                pieces = 2 if len(loaded) == 0 else 1
                width = X_CHUNK_K // pieces
                for i in range(pieces):
                    nc.sync.dma_start(
                        out=buffer[:, i * width : (i + 1) * width],
                        in_=x[m * P : (m + 1) * P, part * X_CHUNK_K + i * width : part * X_CHUNK_K + (i + 1) * width],
                    )
            else:
                buffer = stream.tile([P, W_CHUNK_PASSES, D_HID], U32, name="w1_chunk", tag="stream", align_bytes=64)
                for i in range(W_CHUNK_PASSES):
                    nc.sync.dma_start(
                        out=buffer[:, i, :].bitcast(I32),
                        in_=W1_words[item[1] * W_CHUNK_PASSES + i].rearrange("p n t -> p (n t)").bitcast(I32),
                    )
            loaded[item] = buffer

        u1 = [
            [sums.tile([P, N_PASS], F32, name="u1_%d%d" % (m, h), tag="sum%d%d" % (m, h)) for h in range(HALVES_1)]
            for m in range(TOKEN_TILES)
        ]

        def passes_of_chunk(j, token_tiles):
            for m in token_tiles:
                for i in range(W_CHUNK_PASSES):
                    g = j * W_CHUNK_PASSES + i
                    offset = 4 * (g % PLANES_PER_TILE)
                    for h in range(HALVES_1):
                        features = slice(h * N_PASS, (h + 1) * N_PASS)
                        nc.tensor.matmul_mx(
                            out=u1[m][h][:],
                            lhsT=x_codes[:, m, g * P : (g + 1) * P].bitcast(FP8X4),
                            lhsT_scale=x_scales[:, m, g * P : (g + 1) * P],
                            rhs=loaded[("w", j)][:, i, features].bitcast(FP8X4),
                            rhs_scale=w1_planes[offset:P, g // PLANES_PER_TILE, features],
                            start=(g == 0),
                            stop=(g == PASSES_1 - 1),
                        )

        def repeat_on_all_partitions(block, target, sign, pattern, on_scalar):
            repeated = turn.tile([P, N_PASS], F32, name="repeated", tag="turn")
            for i in range(N_PASS // P):
                row = block * (N_PASS // P) + i
                nc.tensor.matmul(
                    out=repeated[:, i * P : (i + 1) * P],
                    lhsT=ident_bf16[:, row : row + 1].to_broadcast([P, P]),
                    rhs=rows[:],
                    start=True,
                    stop=True,
                )
            dst = target.rearrange("p (t q) -> p t q", t=PACK)
            src = repeated[:].rearrange(pattern, t=PACK)
            if on_scalar:
                nc.scalar.mul(out=dst, in_=src, mul=sign)
            else:
                nc.vector.tensor_scalar_mul(out=dst, in0=src, scalar1=sign)

        with tc.tile_pool(name="stage", bufs=3) as stage:

            def transpose_and_quantise(m, part):
                words = loaded[("x", m, part)][:].bitcast(F32)
                grouped = stage.tile([P, X_CHUNK_K], BF16, name="grouped", align_bytes=64)
                grouped_words = grouped[:].bitcast(F32).rearrange("p (g r u) -> p g r u", g=X_CHUNK_PASSES, u=2)

                def quantise(half):
                    width = X_CHUNK_K // 2
                    first_column = part * X_CHUNK_PASSES * P + half * (width // PACK)
                    columns = slice(first_column, first_column + width // PACK)
                    nc.vector.quantize_mx(
                        out=x_codes[:, m, columns].bitcast(FP8X4),
                        scales=x_scales[:, m, columns],
                        in_=grouped[:, half * width : (half + 1) * width],
                    )

                for bank in range(X_CHUNK_PASSES // BANK_PASSES):
                    turned = turn.tile([P, BANK_PASSES, 2, P], F32, name="turned", tag="turn")
                    for i in range(BANK_PASSES):
                        first_word = (bank * BANK_PASSES + i) * (K_PASS // 2)
                        for u in range(2):
                            nc.tensor.transpose(
                                turned[:, i, u, :], words[:, first_word + u : first_word + K_PASS // 2 : 2], ident_f32[:]
                            )
                    empty_bank(
                        bank,
                        grouped_words[:, bank * BANK_PASSES : (bank + 1) * BANK_PASSES, :, :],
                        turned[:].rearrange("p g u r -> p g r u"),
                    )
                    if bank == 2:
                        quantise(0)
                quantise(1)

            for i in range(STREAM_BUFS):
                load_next()
                if i == 1:
                    load_scales(0, nc.sync, I32)
            for position, item in enumerate(order[: len(order) - TILE_BY_TILE_CHUNKS]):
                if item[0] == "x":
                    transpose_and_quantise(item[1], item[2])
                else:
                    passes_of_chunk(item[1], range(TOKEN_TILES))
                load_next()
                if item == ("w", 2):
                    for h in range(HALVES_1):
                        repeat_on_all_partitions(h, minus_g1_all[:, h, :], -1.0, "p (q t) -> p t q", False)
                        repeat_on_all_partitions(HALVES_1 + h, b1_all[:, h, :], 1.0, "p (q t) -> p t q", True)
                    repeat_on_all_partitions(2 * HALVES_1, minus_g2_all[:], -1.0, "p (t q) -> p t q", False)
                    repeat_on_all_partitions(2 * HALVES_1 + 1, b2_all[:], 1.0, "p (t q) -> p t q", True)

        for m in range(TOKEN_TILES):
            for j in range(W_CHUNKS - TILE_BY_TILE_CHUNKS, W_CHUNKS):
                passes_of_chunk(j, [m])
        nc.sync.dma_start(out=w2_words[:].bitcast(I32), in_=W2_words.rearrange("g p n t -> p g (n t)").bitcast(I32))

        with tc.tile_pool(name="tail", bufs=1) as tail:

            def statistics(name, banks):
                partial = tail.tile([P, len(banks), 6], F32, name="partial_" + name)
                for i, bank in enumerate(banks):
                    nc.vector.bn_stats(out=partial[:, i, :], in_=bank[:])
                mean_var = tail.tile([P, 2], F32, name="mean_var_" + name)
                nc.vector.bn_aggr(out=mean_var[:], in_=partial[:].rearrange("p b s -> p (b s)"))
                return mean_var

            def rstd_on_scalar(name, mean_var):
                rstd = tail.tile([P, 1], F32, name="rstd_" + name)
                nc.scalar.activation(out=rstd[:], in_=mean_var[:, 1:2], func=ACT.Abs_reciprocal_sqrt, bias=eps_col[:])
                return rstd

            def rstd_on_gpsimd(name, mean_var):
                var_eps = tail.tile([P, 1], F32, name="var_eps_" + name)
                nc.vector.tensor_scalar_add(out=var_eps[:], in0=mean_var[:, 1:2], scalar1=EPS)
                rstd = tail.tile([P, 1], F32, name="rstd_" + name)
                nc.gpsimd.tensor_tensor(out=rstd[:], in0=var_eps[:], in1=minus_half[:], op=ALU.pow)
                return rstd

            def centre(piece, mean_var):
                centred = tail.tile([P, PACK, P], F32, name="centred", bufs=2)
                nc.vector.scalar_tensor_tensor(
                    out=centred[:],
                    in0=piece["u"],
                    scalar=mean_var[:, 0:1],
                    in1=piece["minus_gain"],
                    op0=ALU.subtract,
                    op1=ALU.mult,
                )
                piece["centred"] = centred

            def affine_and_exp(piece, rstd):
                minus_v = tail.tile([P, N_PASS], F32, name="minus_v", bufs=4)
                gate = tail.tile([P, N_PASS], F32, name="gate", bufs=4)
                nc.vector.scalar_tensor_tensor(
                    out=minus_v[:],
                    in0=piece["centred"][:].rearrange("p t q -> p (t q)"),
                    scalar=rstd[:],
                    in1=piece["bias"],
                    op0=ALU.mult,
                    op1=ALU.subtract,
                )
                nc.scalar.activation(out=gate[:], in_=minus_v[:], func=ACT.Exp, scale=-1.0)
                piece["minus_v"] = minus_v
                piece["gate"] = gate

            ALL = slice(0, N_PASS)

            def form_n(piece, part=ALL):
                gate = piece["gate"][:, part]
                nc.vector.scalar_tensor_tensor(out=gate, in0=gate, scalar=2.0, in1=gate, op0=ALU.add, op1=ALU.mult)

            def root(piece, part=ALL):
                gate = piece["gate"][:, part]
                nc.scalar.activation(out=gate, in_=gate, func=ACT.Abs_reciprocal_sqrt, bias=two_col[:])

            def square_on_vector(piece, part=ALL):
                gate = piece["gate"][:, part]
                nc.vector.scalar_tensor_tensor(out=gate, in0=gate, scalar=2.0, in1=gate, op0=ALU.mult, op1=ALU.mult)

            def square_on_scalar(piece, part=ALL):
                gate = piece["gate"][:, part]
                nc.scalar.activation(out=gate, in_=gate, func=ACT.Square, scale=SQRT_2)

            def finish(piece, part=ALL):
                nc.vector.scalar_tensor_tensor(
                    out=piece["result"][:, part],
                    in0=piece["gate"][:, part],
                    scalar=1.0,
                    in1=piece["minus_v"][:, part],
                    op0=ALU.subtract,
                    op1=ALU.mult,
                )

            h1 = [tail.tile([P, PASSES_2, PACK, P], BF16, name="h1_%d" % m) for m in range(TOKEN_TILES)]
            pieces_1 = [
                [
                    {
                        "u": u1[m][g][:].rearrange("p (q t) -> p t q", t=PACK),
                        "minus_gain": minus_g1_all[:, g, :].rearrange("p (t q) -> p t q", t=PACK),
                        "bias": b1_all[:, g, :],
                        "result": h1[m][:, g, :, :].rearrange("p t q -> p (t q)"),
                    }
                    for g in range(PASSES_2)
                ]
                for m in range(TOKEN_TILES)
            ]
            mean_var = statistics("10", u1[0])
            rstd = rstd_on_scalar("10", mean_var)
            for piece in pieces_1[0]:
                centre(piece, mean_var)
            for piece in pieces_1[0]:
                affine_and_exp(piece, rstd)
            mean_var = statistics("11", u1[1])
            rstd = rstd_on_gpsimd("11", mean_var)
            for piece in pieces_1[1]:
                centre(piece, mean_var)
            for piece in pieces_1[1]:
                affine_and_exp(piece, rstd)
            for piece in pieces_1[0] + pieces_1[1]:
                form_n(piece)
            for piece in pieces_1[0] + pieces_1[1]:
                root(piece)
            for piece in pieces_1[0]:
                square_on_vector(piece)
            for piece in pieces_1[1]:
                square_on_scalar(piece)
            turned_h = []
            for m in range(TOKEN_TILES):
                for g in range(PASSES_2):
                    finish(pieces_1[m][g])
                    turned = turn.tile([P, PACK, P], BF16, name="turned_h", tag="turn")
                    for t in range(PACK):
                        nc.tensor.transpose(turned[:, t, :], h1[m][:, g, t, :], ident_bf16[:])
                    turned_h.append(turned)

            grouped_h = [
                tail.tile([P, PASSES_2, P, PACK], BF16, name="grouped_h%d" % m, align_bytes=64)
                for m in range(TOKEN_TILES)
            ]
            for i, turned in enumerate(turned_h):
                m, g = divmod(i, PASSES_2)
                empty_bank(i, grouped_h[m][:, g, :, :], turned[:].rearrange("p t r -> p r t"))
            u2 = [sums.tile([P, D_OUT], F32, name="u2_%d" % m, tag="sum%d0" % m) for m in range(TOKEN_TILES)]
            for m in range(TOKEN_TILES):
                for g in range(PASSES_2):
                    tokens = slice(g * P, (g + 1) * P)
                    nc.vector.quantize_mx(
                        out=h_codes[:, m, tokens].bitcast(FP8X4),
                        scales=h_scales[:, m, tokens],
                        in_=grouped_h[m][:, g, :, :].rearrange("p r t -> p (r t)"),
                    )
                    nc.tensor.matmul_mx(
                        out=u2[m][:],
                        lhsT=h_codes[:, m, tokens].bitcast(FP8X4),
                        lhsT_scale=h_scales[:, m, tokens],
                        rhs=w2_words[:, g, :].bitcast(FP8X4),
                        rhs_scale=w2_planes[4 * g : P, :],
                        start=(g == 0),
                        stop=(g == PASSES_2 - 1),
                    )

            mish_2 = [tail.tile([P, D_OUT], F32, name="mish_2_%d" % m) for m in range(TOKEN_TILES)]
            pieces_2 = [
                {
                    "u": u2[m][:].rearrange("p (t q) -> p t q", t=PACK),
                    "minus_gain": minus_g2_all[:].rearrange("p (t q) -> p t q", t=PACK),
                    "bias": b2_all[:],
                    "result": mish_2[m][:],
                }
                for m in range(TOKEN_TILES)
            ]
            mean_vars = [statistics("2%d" % m, [u2[m]]) for m in range(TOKEN_TILES)]
            rstds = [rstd_on_scalar("2%d" % m, mean_vars[m]) for m in range(TOKEN_TILES)]
            for m, piece in enumerate(pieces_2):
                centre(piece, mean_vars[m])
            for m, piece in enumerate(pieces_2):
                affine_and_exp(piece, rstds[m])
            for piece in pieces_2:
                form_n(piece)
            halves = [slice(0, N_PASS // 2), slice(N_PASS // 2, N_PASS)]
            root(pieces_2[0])
            for half in halves:
                root(pieces_2[1], half)
            square_on_vector(pieces_2[0])
            square_on_vector(pieces_2[1], halves[0])
            square_on_scalar(pieces_2[1], halves[1])
            finish(pieces_2[0])
            nc.sync.dma_start(out=out[0:P, :], in_=mish_2[0][:])
            for half, queue in zip(halves, (nc.scalar, nc.sync)):
                finish(pieces_2[1], half)
                queue.dma_start(out=out[P : 2 * P, half], in_=mish_2[1][:, half])
